import numpy as np
import ml_dtypes


def mxq(x, axis, fmt="e4m3"):
    dtype, down = {"e4m3": (ml_dtypes.float8_e4m3fn, 7), "e5m2": (ml_dtypes.float8_e5m2, 14)}[fmt]
    v = np.moveaxis(np.asarray(x, np.float32).astype(ml_dtypes.bfloat16).astype(np.float64), axis, -1)
    blocks = v.reshape(v.shape[:-1] + (-1, 32))
    amax = np.abs(blocks).max(-1, keepdims=True)
    byte = np.maximum(np.where(amax > 0, np.frexp(amax)[1] - 1 + 127, 0) - down, 1)
    scale = np.exp2(byte - 127.0)
    codes = (blocks / scale).astype(np.float32).astype(dtype).astype(np.float64)
    return np.moveaxis((codes * scale).reshape(v.shape), -1, axis)


WIDE = False


def mx_kscale(k):
    if not WIDE:
        return np.ones(k)
    levels = np.array([10, -10, 5, -5, 0])
    if k % 512:
        return np.exp2(np.random.permutation(np.resize(levels, k // 32))).repeat(32)
    a = np.empty((k // 512, 16))
    for p in range(k // 512):
        a[p, :8] = np.random.permutation(np.resize(levels, 8))
        for g in range(8):
            far = levels[np.abs(levels - a[p, g]) >= 10]
            a[p, g + 8] = far[np.random.randint(len(far))]
    return np.exp2(a.ravel()).repeat(32)


BF16 = ml_dtypes.bfloat16


def bf(x):
    return np.asarray(x, np.float32).astype(BF16)


def f64(x):
    return np.asarray(x).astype(np.float64)


B, A, C, D, K0, K1, K2 = 2, 128, 64, 512, 512, 128, 256
D2 = D + D
NEG_SLOPE = 0.01


def leaky(v):
    return np.where(v >= 0, v, NEG_SLOPE * v)


def draw0():
    s, t = mx_kscale(D), mx_kscale(K0)
    ss = np.concatenate([s, s])
    return {"sent_a": bf(np.random.standard_normal((B, A, D)) * s),
            "sent_b": bf(np.random.standard_normal((B, C, D)) * s),
            "W1": bf(np.random.standard_normal((D2, K0)) / np.sqrt(D2) / ss[:, None] * t),
            "b1": bf((np.random.standard_normal(K0) * 0.5 - 0.5) * t),
            "W2": bf(np.random.standard_normal((K0, K1)) * 2.0 / np.sqrt(K0) / t[:, None]),
            "b2": bf(np.random.standard_normal(K1) * 0.5 - 0.5)}


def core(sent_a, sent_b, W1, b1, W2, b2):
    w1 = f64(W1)
    a_part = mxq(f64(sent_a), 2, "e4m3") @ mxq(w1[:D], 0, "e4m3")
    b_part = mxq(f64(sent_b), 2, "e4m3") @ mxq(w1[D:], 0, "e4m3")
    h = leaky(a_part[:, :, None, :] + b_part[:, None, :, :] + f64(b1))
    return leaky((mxq(h, 3, "e4m3") @ mxq(f64(W2), 0, "e4m3")) + f64(b2))


def e4m3fn_bytes(y):
    return np.clip(np.asarray(y, np.float64), -448.0, 448.0).astype(np.float32).astype(ml_dtypes.float8_e4m3fn).view(np.uint8)


def e4m3fn_values(b):
    return np.asarray(b, np.uint8).view(ml_dtypes.float8_e4m3fn).astype(np.float64)


def setup_inputs():
    d = draw0()
    x0 = np.asarray(d['sent_a']).astype(np.float64)
    s = (np.max(np.abs(x0), axis=(0, 1), keepdims=True) / 448.0).astype(np.float32)
    out = {}
    for k, v in d.items():
        if k == 'sent_a':
            out['sent_a_bytes'] = e4m3fn_bytes(x0 / s.astype(np.float64))
            out['sent_a_scale'] = s
        else:
            out[k] = v
    return out


def reference(sent_a_bytes, sent_a_scale, sent_b, W1, b1, W2, b2):
    return core(e4m3fn_values(sent_a_bytes) * sent_a_scale.astype(np.float64), sent_b, W1, b1, W2, b2)

@@ -1,0 +1,241 @@
+from contextlib import ExitStack
+
+import concourse.mybir as mybir
+from concourse.masks import make_identity
+
+B, A, C, D, K0, K1 = 2, 128, 64, 512, 512, 128
+FLOPS = 2 * B * A * C * K0 * K1 + 2 * B * A * D * K0 + 2 * B * C * D * K0
+
+F32 = mybir.dt.float32
+BF16 = mybir.dt.bfloat16
+U32 = mybir.dt.uint32
+U8 = mybir.dt.uint8
+FP8 = mybir.dt.float8_e4m3fn
+FP8X4 = mybir.dt.float8_e4m3fn_x4
+ACT = mybir.ActivationFunctionType
+ALU = mybir.AluOpType
+
+P = 128
+T = 4
+JB = 4
+GROUPS_PER_N = C // JB
+GROUPS = B * GROUPS_PER_N
+COLS = JB * A
+V_PLANES = 2
+
+
+def tile_matchmatrix_pa_t_kernel(tc, sent_a_bytes, sent_a_scale, sent_b, W1, b1, W2, b2, out):
+    nc = tc.nc
+    with ExitStack() as ctx:
+        keep = ctx.enter_context(tc.tile_pool(name="keep", bufs=1))
+        head = ctx.enter_context(tc.tile_pool(name="head", bufs=4))
+        work = ctx.enter_context(tc.tile_pool(name="work", bufs=3))
+        psum = ctx.enter_context(tc.psum_pool(name="psum", bufs=2))
+
+        a_bytes = keep.tile([P, B, D], U8, align_bytes=64)
+        b_rows = keep.tile([P, D], BF16, align_bytes=64)
+        a_scale = keep.tile([P, T], F32)
+        wb_raw = keep.tile([P, T, K0], BF16, align_bytes=64)
+        wa_raw = keep.tile([P, T, K0], BF16, align_bytes=64)
+        w2_raw = keep.tile([P, T, K1], BF16, align_bytes=64)
+        b1c = keep.tile([P, T], BF16)
+        b2c = keep.tile([P, 1], BF16)
+        ident = keep.tile([P, P], F32, align_bytes=64)
+        warm = keep.tile([P, 1], F32)
+
+        a_wide = keep.tile([P, B, D], BF16, align_bytes=64)
+        a_grp = keep.tile([P, B, A, T], BF16, align_bytes=64)
+        b_grp = keep.tile([P, P, T], BF16, align_bytes=64)
+        a_codes = keep.tile([P, B * A], U32, align_bytes=64)
+        a_scl = keep.tile([P, B * A], U8, align_bytes=64)
+        b_codes = keep.tile([P, P], U32, align_bytes=64)
+        b_scl = keep.tile([P, P], U8, align_bytes=64)
+        w2_grp = keep.tile([P, K1, T], BF16, align_bytes=64)
+        w2_codes = keep.tile([P, K1], U32, align_bytes=64)
+        w2_scl = keep.tile([P, K1], U8, align_bytes=64)
+        bp = []
+        ap_sb = []
+        for t in range(T):
+            bp.append(keep.tile([P, B * C], F32, align_bytes=64, name="bp" + str(t)))
+            ap_sb.append(keep.tile([P, B * A], F32, align_bytes=64, name="ap" + str(t)))
+
+        with tc.manual_schedule():
+            nc.sync.dma_start(out=a_bytes[:], in_=sent_a_bytes.rearrange("n i k -> i n k"))
+            nc.sync.dma_start(out=b_rows[:], in_=sent_b.rearrange("n j k -> (n j) k"))
+            nc.sync.dma_start(out=wb_raw[:], in_=W1[D : 2 * D, :].rearrange("(p j) c -> p j c", j=T))
+            nc.sync.dma_start(out=wa_raw[:], in_=W1[0:D, :].rearrange("(p j) c -> p j c", j=T))
+            nc.sync.dma_start(out=w2_raw[:], in_=W2.rearrange("(p j) e -> p j e", j=T))
+            nc.scalar.dma_start(out=a_scale[:], in_=sent_a_scale.rearrange("x y (p t) -> p (x y t)", t=T))
+            nc.scalar.dma_start(out=b1c[:], in_=b1.rearrange("(p t) -> p t", t=T))
+            nc.scalar.dma_start(out=b2c[:], in_=b2.rearrange("(e o) -> e o", o=1))
+            nc.vector.memset(warm[:], 0.0)
+            nc.scalar.activation(out=warm[:], in_=warm[:], func=ACT.Identity)
+            make_identity(nc, ident[:])
+
+            def widen(n, engine):
+                if engine == "v":
+                    nc.vector.tensor_copy(out=a_wide[:, n, :], in_=a_bytes[:, n, :].bitcast(FP8))
+                else:
+                    nc.scalar.activation(out=a_wide[:, n, :], in_=a_bytes[:, n, :].bitcast(FP8), func=ACT.Copy)
+
+            at_ps = psum.tile([P, B, 2, A], F32, tag="t")
+            bt_ps = psum.tile([P, 2, P], F32, tag="t")
+            widen(0, "v")
+            widen(1, "s")
+            a_words = a_wide[:].bitcast(F32)
+            b_words = b_rows[:].bitcast(F32)
+            for u in range(2):
+                nc.tensor.transpose(bt_ps[:, u, :], b_words[:, u : D // 2 : 2], ident[:])
+            for n in range(B):
+                for u in range(2):
+                    nc.tensor.transpose(at_ps[:, n, u, :], a_words[:, n, u : D // 2 : 2], ident[:])
+            nc.scalar.copy(
+                out=b_grp[:].rearrange("p r t -> p (r t)").bitcast(F32).rearrange("p (r u) -> p r u", u=2),
+                in_=bt_ps[:].rearrange("p u r -> p r u"),
+            )
+            for n in range(B):
+                nc.vector.tensor_tensor(
+                    out=a_grp[:, n].rearrange("p i (u e) -> p i u e", u=2),
+                    in0=at_ps[:, n].bitcast(BF16).rearrange("p u (i e) -> p i u e", e=2),
+                    in1=a_scale[:].rearrange("p (u e) -> p u e", u=2).unsqueeze(1).to_broadcast([P, A, 2, 2]),
+                    op=ALU.mult,
+                )
+            nc.vector.quantize_mx(
+                out=b_codes[:].bitcast(FP8X4), scales=b_scl[:], in_=b_grp[:].rearrange("p r t -> p (r t)")
+            )
+            nc.vector.quantize_mx(
+                out=a_codes[:].bitcast(FP8X4), scales=a_scl[:], in_=a_grp[:].rearrange("p n i t -> p (n i t)")
+            )
+
+            a_ps = []
+            b_ps = psum.tile([P, T, B * C], F32, tag="x", bufs=3)
+            for h in range(2):
+                a_ps.append(psum.tile([P, 2, B * A], F32, tag="x", bufs=3, name="a_ps" + str(h)))
+
+            def b_bias(t):
+                nc.vector.tensor_scalar(
+                    out=bp[t][:], in0=b_ps[:, t, :], scalar1=b1c[:, t : t + 1], scalar2=None, op0=ALU.add
+                )
+
+            def a_copy(t):
+                nc.scalar.copy(out=ap_sb[t][:], in_=a_ps[t // 2][:, t % 2, :])
+
+            for t in range(T):
+                wb_grp = head.tile([P, P, T], BF16, align_bytes=64)
+                wa_grp = head.tile([P, P, T], BF16, align_bytes=64)
+                nc.scalar.copy(out=wb_grp[:], in_=wb_raw[:].rearrange("p j (m t) -> p t m j", t=T)[:, t])
+                nc.vector.tensor_copy(out=wa_grp[:], in_=wa_raw[:].rearrange("p j (m t) -> p t m j", t=T)[:, t])
+                wb_codes = head.tile([P, P], U32, align_bytes=64)
+                wb_scl = head.tile([P, P], U8, align_bytes=64)
+                wa_codes = head.tile([P, P], U32, align_bytes=64)
+                wa_scl = head.tile([P, P], U8, align_bytes=64)
+                nc.vector.quantize_mx(
+                    out=wb_codes[:].bitcast(FP8X4), scales=wb_scl[:], in_=wb_grp[:].rearrange("p m j -> p (m j)")
+                )
+                nc.vector.quantize_mx(
+                    out=wa_codes[:].bitcast(FP8X4), scales=wa_scl[:], in_=wa_grp[:].rearrange("p m j -> p (m j)")
+                )
+                nc.tensor.matmul_mx(
+                    out=b_ps[:, t, :],
+                    lhsT=wb_codes[:].bitcast(FP8X4),
+                    lhsT_scale=wb_scl[:],
+                    rhs=b_codes[:].bitcast(FP8X4),
+                    rhs_scale=b_scl[:],
+                    start=True,
+                    stop=True,
+                )
+                nc.tensor.matmul_mx(
+                    out=a_ps[t // 2][:, t % 2, :],
+                    lhsT=wa_codes[:].bitcast(FP8X4),
+                    lhsT_scale=wa_scl[:],
+                    rhs=a_codes[:].bitcast(FP8X4),
+                    rhs_scale=a_scl[:],
+                    start=True,
+                    stop=True,
+                )
+                if t > 0:
+                    b_bias(t - 1)
+                    a_copy(t - 1)
+            b_bias(T - 1)
+            a_copy(T - 1)
+
+            def pair_planes(g, v):
+                n, j0 = g // GROUPS_PER_N, (g % GROUPS_PER_N) * JB
+                for t in range(T):
+                    for jj in range(JB):
+                        bias = bp[t][:, n * C + j0 + jj : n * C + j0 + jj + 1]
+                        src = ap_sb[t][:, n * A : (n + 1) * A]
+                        dst = v[:, t, jj * A : (jj + 1) * A]
+                        if t * JB + jj >= T * JB - V_PLANES:
+                            nc.vector.tensor_scalar(out=dst, in0=src, scalar1=bias, scalar2=None, op0=ALU.add)
+                        else:
+                            nc.scalar.activation(out=dst, in_=src, func=ACT.Identity, bias=bias)
+
+            def new_planes(g):
+                v = work.tile([P, T, COLS], F32, align_bytes=64, name="v")
+                pair_planes(g, v)
+                return v
+
+            planes = {}
+            planes[0] = new_planes(0)
+            nc.vector.tensor_copy(out=w2_grp[:], in_=w2_raw[:].rearrange("p j e -> p e j"))
+            planes[1] = new_planes(1)
+            nc.vector.quantize_mx(
+                out=w2_codes[:].bitcast(FP8X4), scales=w2_scl[:], in_=w2_grp[:].rearrange("p e j -> p (e j)")
+            )
+
+            x_of = {}
+            y_of = {}
+            o_of = {}
+            for g in range(GROUPS + 2):
+                if g >= 2:
+                    o_sb = work.tile([P, JB, K1], F32, align_bytes=64)
+                    nc.scalar.copy(out=o_sb[:], in_=o_of[g - 2][:])
+                    n, j0 = (g - 2) // GROUPS_PER_N, ((g - 2) % GROUPS_PER_N) * JB
+                    nc.sync.dma_start(out=out[n, :, j0 : j0 + JB, :], in_=o_sb[:])
+                if 1 <= g <= GROUPS:
+                    y = work.tile([P, COLS], F32, align_bytes=64)
+                    nc.scalar.activation(out=y[:], in_=x_of[g - 1][:], func=ACT.Identity, bias=b2c[:])
+                    y_of[g - 1] = y
+                if g < GROUPS:
+                    h = work.tile([P, COLS, T], BF16, align_bytes=64)
+                    v_view = planes[g][:].rearrange("p t c -> p c t")
+                    nc.vector.scalar_tensor_tensor(
+                        out=h[:], in0=v_view, scalar=0.01, in1=v_view, op0=ALU.mult, op1=ALU.max
+                    )
+                if 1 <= g <= GROUPS:
+                    r = work.tile([P, COLS], F32, align_bytes=64)
+                    nc.vector.tensor_scalar(
+                        out=r[:], in0=y_of[g - 1][:], scalar1=0.0, scalar2=-0.99, op0=ALU.min, op1=ALU.mult
+                    )
+                if g + 2 < GROUPS:
+                    planes[g + 2] = new_planes(g + 2)
+                if g < GROUPS:
+                    h_codes = work.tile([P, COLS], U32, align_bytes=64)
+                    h_scl = work.tile([P, COLS], U8, align_bytes=64)
+                    nc.vector.quantize_mx(
+                        out=h_codes[:].bitcast(FP8X4), scales=h_scl[:], in_=h[:].rearrange("p c t -> p (c t)")
+                    )
+                if 1 <= g <= GROUPS:
+                    o = psum.tile([P, JB, K1], F32, tag="t")
+                    for jj in range(JB):
+                        cols = slice(jj * A, (jj + 1) * A)
+                        nc.tensor.matmul(
+                            o[:, jj, :], lhsT=y_of[g - 1][:, cols], rhs=ident[:], start=True, stop=False, is_transpose=True
+                        )
+                        nc.tensor.matmul(
+                            o[:, jj, :], lhsT=r[:, cols], rhs=ident[:], start=False, stop=True, is_transpose=True
+                        )
+                    o_of[g - 1] = o
+                if g < GROUPS:
+                    x = psum.tile([P, COLS], F32, tag="x", bufs=3)
+                    nc.tensor.matmul_mx(
+                        out=x[:],
+                        lhsT=w2_codes[:].bitcast(FP8X4),
+                        lhsT_scale=w2_scl[:],
+                        rhs=h_codes[:].bitcast(FP8X4),
+                        rhs_scale=h_scl[:],
+                        start=True,
+                        stop=True,
+                    )
+                    x_of[g] = x

@@ -21,7 +21,9 @@ JB = 4
 GROUPS_PER_N = C // JB
 GROUPS = B * GROUPS_PER_N
 COLS = JB * A
-V_PLANES = 2
+W_J = 2
+Z_J = JB - W_J
+I4 = 4
 
 
 def tile_matchmatrix_pa_t_kernel(tc, sent_a_bytes, sent_a_scale, sent_b, W1, b1, W2, b2, out):
@@ -53,11 +55,17 @@ def tile_matchmatrix_pa_t_kernel(tc, sent_a_bytes, sent_a_scale, sent_b, W1, b1,
         w2_grp = keep.tile([P, K1, T], BF16, align_bytes=64)
         w2_codes = keep.tile([P, K1], U32, align_bytes=64)
         w2_scl = keep.tile([P, K1], U8, align_bytes=64)
+        b2n = keep.tile([P, 1], F32)
         bp = []
-        ap_sb = []
+        nb = []
+        t01 = []
+        t99 = []
         for t in range(T):
             bp.append(keep.tile([P, B * C], F32, align_bytes=64, name="bp" + str(t)))
-            ap_sb.append(keep.tile([P, B * A], F32, align_bytes=64, name="ap" + str(t)))
+            nb.append(keep.tile([P, B * C], F32, align_bytes=64, name="nb" + str(t)))
+        for n in range(B):
+            t01.append(keep.tile([P, T, A], F32, align_bytes=64, name="t01_" + str(n)))
+            t99.append(keep.tile([P, T, A], F32, align_bytes=64, name="t99_" + str(n)))
 
         with tc.manual_schedule():
             nc.sync.dma_start(out=a_bytes[:], in_=sent_a_bytes.rearrange("n i k -> i n k"))
@@ -78,8 +86,8 @@ def tile_matchmatrix_pa_t_kernel(tc, sent_a_bytes, sent_a_scale, sent_b, W1, b1,
                 else:
                     nc.scalar.activation(out=a_wide[:, n, :], in_=a_bytes[:, n, :].bitcast(FP8), func=ACT.Copy)
 
-            at_ps = psum.tile([P, B, 2, A], F32, tag="t")
-            bt_ps = psum.tile([P, 2, P], F32, tag="t")
+            at_ps = psum.tile([P, B, 2, A], F32, tag="wd")
+            bt_ps = psum.tile([P, 2, P], F32, tag="wd")
             widen(0, "v")
             widen(1, "s")
             a_words = a_wide[:].bitcast(F32)
@@ -107,18 +115,15 @@ def tile_matchmatrix_pa_t_kernel(tc, sent_a_bytes, sent_a_scale, sent_b, W1, b1,
                 out=a_codes[:].bitcast(FP8X4), scales=a_scl[:], in_=a_grp[:].rearrange("p n i t -> p (n i t)")
             )
 
+            nc.vector.tensor_scalar(out=b2n[:], in0=b2c[:], scalar1=-0.99, scalar2=None, op0=ALU.mult)
+            b_ps = psum.tile([P, T, B * C], F32, tag="x")
             a_ps = []
-            b_ps = psum.tile([P, T, B * C], F32, tag="x", bufs=3)
-            for h in range(2):
-                a_ps.append(psum.tile([P, 2, B * A], F32, tag="x", bufs=3, name="a_ps" + str(h)))
+            for n in range(B):
+                a_ps.append(psum.tile([P, T, A], F32, tag="o", name="a_ps" + str(n)))
 
-            def b_bias(t):
-                nc.vector.tensor_scalar(
-                    out=bp[t][:], in0=b_ps[:, t, :], scalar1=b1c[:, t : t + 1], scalar2=None, op0=ALU.add
-                )
-
-            def a_copy(t):
-                nc.scalar.copy(out=ap_sb[t][:], in_=a_ps[t // 2][:, t % 2, :])
+            def bias(t):
+                nc.scalar.activation(out=bp[t][:], in_=b_ps[:, t, :], func=ACT.Identity, bias=b1c[:, t : t + 1])
+                nc.vector.tensor_scalar(out=nb[t][:], in0=bp[t][:], scalar1=-0.99, scalar2=None, op0=ALU.mult)
 
             for t in range(T):
                 wb_grp = head.tile([P, P, T], BF16, align_bytes=64)
@@ -144,91 +149,142 @@ def tile_matchmatrix_pa_t_kernel(tc, sent_a_bytes, sent_a_scale, sent_b, W1, b1,
                     start=True,
                     stop=True,
                 )
-                nc.tensor.matmul_mx(
-                    out=a_ps[t // 2][:, t % 2, :],
-                    lhsT=wa_codes[:].bitcast(FP8X4),
-                    lhsT_scale=wa_scl[:],
-                    rhs=a_codes[:].bitcast(FP8X4),
-                    rhs_scale=a_scl[:],
-                    start=True,
-                    stop=True,
-                )
-                if t > 0:
-                    b_bias(t - 1)
-                    a_copy(t - 1)
-            b_bias(T - 1)
-            a_copy(T - 1)
-
-            def pair_planes(g, v):
-                n, j0 = g // GROUPS_PER_N, (g % GROUPS_PER_N) * JB
-                for t in range(T):
-                    for jj in range(JB):
-                        bias = bp[t][:, n * C + j0 + jj : n * C + j0 + jj + 1]
-                        src = ap_sb[t][:, n * A : (n + 1) * A]
-                        dst = v[:, t, jj * A : (jj + 1) * A]
-                        if t * JB + jj >= T * JB - V_PLANES:
-                            nc.vector.tensor_scalar(out=dst, in0=src, scalar1=bias, scalar2=None, op0=ALU.add)
-                        else:
-                            nc.scalar.activation(out=dst, in_=src, func=ACT.Identity, bias=bias)
-
-            def new_planes(g):
-                v = work.tile([P, T, COLS], F32, align_bytes=64, name="v")
-                pair_planes(g, v)
-                return v
-
-            planes = {}
-            planes[0] = new_planes(0)
+                for n in range(B):
+                    nc.tensor.matmul_mx(
+                        out=a_ps[n][:, t, :],
+                        lhsT=wa_codes[:].bitcast(FP8X4),
+                        lhsT_scale=wa_scl[:],
+                        rhs=a_codes[:, n * A : (n + 1) * A].bitcast(FP8X4),
+                        rhs_scale=a_scl[:, n * A : (n + 1) * A],
+                        start=True,
+                        stop=True,
+                    )
+            for t in range(T):
+                bias(t)
+            for n in range(B):
+                nc.scalar.activation(out=t99[n][:], in_=a_ps[n][:], func=ACT.Copy, scale=0.99)
+                nc.scalar.activation(out=t01[n][:], in_=a_ps[n][:], func=ACT.Copy, scale=0.01)
             nc.vector.tensor_copy(out=w2_grp[:], in_=w2_raw[:].rearrange("p j e -> p e j"))
-            planes[1] = new_planes(1)
             nc.vector.quantize_mx(
                 out=w2_codes[:].bitcast(FP8X4), scales=w2_scl[:], in_=w2_grp[:].rearrange("p e j -> p (e j)")
             )
 
+            def place(g):
+                return g // GROUPS_PER_N, (g % GROUPS_PER_N) * JB
+
+            def planes(g, jj0, count, tile):
+                n, j0 = place(g)
+                for jj in range(count):
+                    col = slice(n * C + j0 + jj0 + jj, n * C + j0 + jj0 + jj + 1)
+                    for t in range(T):
+                        nc.vector.tensor_scalar(
+                            out=tile[:, t, jj * A : (jj + 1) * A],
+                            in0=t99[n][:, t, :],
+                            scalar1=nb[t][:, col],
+                            scalar2=bp[t][:, col],
+                            op0=ALU.max,
+                            op1=ALU.add,
+                        )
+
+            wz_of = {}
+            hz_of = {}
+            h_of = {}
             x_of = {}
-            y_of = {}
+            yr_of = {}
             o_of = {}
-            for g in range(GROUPS + 2):
-                if g >= 2:
+
+            def valid(g):
+                return 0 <= g < GROUPS
+
+            def z_planes(g):
+                wz = work.tile([P, T, Z_J * A], F32, align_bytes=64)
+                planes(g, W_J, Z_J, wz)
+                wz_of[g] = wz
+
+            def z_add(g, jz):
+                n = place(g)[0]
+                hz_ps = psum.tile([P, T, P], F32, tag="hz")
+                cols = slice(jz * A, (jz + 1) * A)
+                for t in range(T):
+                    nc.tensor.matmul(
+                        hz_ps[:, t, :], lhsT=wz_of[g][:, t, cols], rhs=ident[:], start=True, stop=False, is_transpose=True
+                    )
+                    nc.tensor.matmul(
+                        hz_ps[:, t, :], lhsT=t01[n][:, t, :], rhs=ident[:], start=False, stop=True, is_transpose=True
+                    )
+                return hz_ps
+
+            def z_round(g, jz, hz_ps):
+                hz = work.tile([P, 2, P, 2], BF16, align_bytes=64, tag="hz", bufs=6)
+                nc.scalar.copy(out=hz[:], in_=hz_ps[:].rearrange("i (u e) m -> i u m e", e=2))
+                hz_of[g, jz] = hz
+
+            def z_back(g):
+                wd_ps = psum.tile([P, Z_J, 2, A], F32, tag="wd")
+                for jz in range(Z_J):
+                    words = hz_of[g, jz][:].rearrange("i u m e -> i (u m e)").bitcast(F32)
+                    for u in range(2):
+                        nc.tensor.transpose(wd_ps[:, jz, u, :], words[:, u * P : (u + 1) * P], ident[:])
+                return wd_ps
+
+            def z_copy(g, wd_ps):
+                h_words = h_of[g][:, W_J * A :, :].rearrange("p c t -> p (c t)").bitcast(F32)
+                nc.scalar.copy(
+                    out=h_words.rearrange("p (j i u) -> p j i u", j=Z_J, u=2),
+                    in_=wd_ps[:].rearrange("p j u i -> p j i u"),
+                )
+
+            def w_add(g, ww):
+                n = place(g)[0]
+                for jj in range(W_J):
+                    cols = slice(jj * A, (jj + 1) * A)
+                    nc.vector.tensor_tensor(
+                        out=h_of[g][:, cols, :].rearrange("p (c i) t -> p c t i", i=I4),
+                        in0=t01[n][:].rearrange("p t (c i) -> p c t i", i=I4),
+                        in1=ww[:, :, cols].rearrange("p t (c i) -> p c t i", i=I4),
+                        op=ALU.add,
+                    )
+
+            def out_transposes(g):
+                y, r = yr_of[g]
+                o = psum.tile([P, JB, K1], F32, tag="o")
+                for jj in range(JB):
+                    cols = slice(jj * A, (jj + 1) * A)
+                    nc.tensor.matmul(
+                        o[:, jj, :], lhsT=y[:, cols], rhs=ident[:], start=True, stop=False, is_transpose=True
+                    )
+                    nc.tensor.matmul(
+                        o[:, jj, :], lhsT=r[:, cols], rhs=ident[:], start=False, stop=True, is_transpose=True
+                    )
+                o_of[g] = o
+
+            for g in range(-2, GROUPS + 3):
+                if valid(g - 3):
                     o_sb = work.tile([P, JB, K1], F32, align_bytes=64)
-                    nc.scalar.copy(out=o_sb[:], in_=o_of[g - 2][:])
-                    n, j0 = (g - 2) // GROUPS_PER_N, ((g - 2) % GROUPS_PER_N) * JB
+                    nc.scalar.copy(out=o_sb[:], in_=o_of[g - 3][:])
+                    n, j0 = place(g - 3)
                     nc.sync.dma_start(out=out[n, :, j0 : j0 + JB, :], in_=o_sb[:])
-                if 1 <= g <= GROUPS:
-                    y = work.tile([P, COLS], F32, align_bytes=64)
-                    nc.scalar.activation(out=y[:], in_=x_of[g - 1][:], func=ACT.Identity, bias=b2c[:])
-                    y_of[g - 1] = y
-                if g < GROUPS:
+                if valid(g):
                     h = work.tile([P, COLS, T], BF16, align_bytes=64)
-                    v_view = planes[g][:].rearrange("p t c -> p c t")
-                    nc.vector.scalar_tensor_tensor(
-                        out=h[:], in0=v_view, scalar=0.01, in1=v_view, op0=ALU.mult, op1=ALU.max
-                    )
-                if 1 <= g <= GROUPS:
+                    h_of[g] = h
+                    z_copy(g, z_back(g))
+                if valid(g + 2):
+                    z_planes(g + 2)
+                if valid(g - 2):
+                    y = work.tile([P, COLS], F32, align_bytes=64)
+                    nc.scalar.activation(out=y[:], in_=x_of[g - 2][:], func=ACT.Identity, bias=b2c[:])
                     r = work.tile([P, COLS], F32, align_bytes=64)
-                    nc.vector.tensor_scalar(
-                        out=r[:], in0=y_of[g - 1][:], scalar1=0.0, scalar2=-0.99, op0=ALU.min, op1=ALU.mult
-                    )
-                if g + 2 < GROUPS:
-                    planes[g + 2] = new_planes(g + 2)
-                if g < GROUPS:
+                    nc.scalar.activation(out=r[:], in_=x_of[g - 2][:], func=ACT.Relu, bias=b2n[:], scale=-0.99)
+                    yr_of[g - 2] = (y, r)
+                if valid(g + 1):
+                    z_round(g + 1, 0, z_add(g + 1, 0))
+                if valid(g - 1):
                     h_codes = work.tile([P, COLS], U32, align_bytes=64)
                     h_scl = work.tile([P, COLS], U8, align_bytes=64)
                     nc.vector.quantize_mx(
-                        out=h_codes[:].bitcast(FP8X4), scales=h_scl[:], in_=h[:].rearrange("p c t -> p (c t)")
+                        out=h_codes[:].bitcast(FP8X4), scales=h_scl[:], in_=h_of[g - 1][:].rearrange("p c t -> p (c t)")
                     )
-                if 1 <= g <= GROUPS:
-                    o = psum.tile([P, JB, K1], F32, tag="t")
-                    for jj in range(JB):
-                        cols = slice(jj * A, (jj + 1) * A)
-                        nc.tensor.matmul(
-                            o[:, jj, :], lhsT=y_of[g - 1][:, cols], rhs=ident[:], start=True, stop=False, is_transpose=True
-                        )
-                        nc.tensor.matmul(
-                            o[:, jj, :], lhsT=r[:, cols], rhs=ident[:], start=False, stop=True, is_transpose=True
-                        )
-                    o_of[g - 1] = o
-                if g < GROUPS:
-                    x = psum.tile([P, COLS], F32, tag="x", bufs=3)
+                    x = psum.tile([P, COLS], F32, tag="x")
                     nc.tensor.matmul_mx(
                         out=x[:],
                         lhsT=w2_codes[:].bitcast(FP8X4),
@@ -238,4 +294,12 @@ def tile_matchmatrix_pa_t_kernel(tc, sent_a_bytes, sent_a_scale, sent_b, W1, b1,
                         start=True,
                         stop=True,
                     )
-                    x_of[g] = x
+                    x_of[g - 1] = x
+                if valid(g + 1):
+                    z_round(g + 1, 1, z_add(g + 1, 1))
+                if valid(g):
+                    ww = work.tile([P, T, W_J * A], F32, align_bytes=64)
+                    planes(g, 0, W_J, ww)
+                    w_add(g, ww)
+                if valid(g - 2):
+                    out_transposes(g - 2)

@@ -17,13 +17,24 @@ ALU = mybir.AluOpType
 
 P = 128
 T = 4
-JB = 4
-GROUPS_PER_N = C // JB
-GROUPS = B * GROUPS_PER_N
-COLS = JB * A
-W_J = 2
-Z_J = JB - W_J
 I4 = 4
+MIXES = {1: [(1, 0, 0)], 2: [(1, 1, 0)], 4: [(2, 1, 1), (1, 2, 1)]}
+
+
+def group_list():
+    groups = []
+    for n in range(B):
+        sizes = [4] * 15
+        sizes = [1, 1, 2] + sizes if n == 0 else sizes + [2, 1, 1]
+        j = 0
+        for i, size in enumerate(sizes):
+            mixes = MIXES[size]
+            groups.append((n, j, size) + mixes[i % len(mixes)])
+            j += size
+    return groups
+
+
+GROUPS = group_list()
 
 
 def tile_matchmatrix_pa_t_kernel(tc, sent_a_bytes, sent_a_scale, sent_b, W1, b1, W2, b2, out):
@@ -86,8 +97,8 @@ def tile_matchmatrix_pa_t_kernel(tc, sent_a_bytes, sent_a_scale, sent_b, W1, b1,
                 else:
                     nc.scalar.activation(out=a_wide[:, n, :], in_=a_bytes[:, n, :].bitcast(FP8), func=ACT.Copy)
 
-            at_ps = psum.tile([P, B, 2, A], F32, tag="wd")
-            bt_ps = psum.tile([P, 2, P], F32, tag="wd")
+            at_ps = psum.tile([P, B, 2, A], F32, tag="hz")
+            bt_ps = psum.tile([P, 2, P], F32, tag="hz")
             widen(0, "v")
             widen(1, "s")
             a_words = a_wide[:].bitcast(F32)
@@ -169,13 +180,13 @@ def tile_matchmatrix_pa_t_kernel(tc, sent_a_bytes, sent_a_scale, sent_b, W1, b1,
                 out=w2_codes[:].bitcast(FP8X4), scales=w2_scl[:], in_=w2_grp[:].rearrange("p e j -> p (e j)")
             )
 
-            def place(g):
-                return g // GROUPS_PER_N, (g % GROUPS_PER_N) * JB
+            def valid(g):
+                return 0 <= g < len(GROUPS)
 
-            def planes(g, jj0, count, tile):
-                n, j0 = place(g)
+            def max_add_planes(g, first, count, tile):
+                n, j0 = GROUPS[g][0:2]
                 for jj in range(count):
-                    col = slice(n * C + j0 + jj0 + jj, n * C + j0 + jj0 + jj + 1)
+                    col = slice(n * C + j0 + first + jj, n * C + j0 + first + jj + 1)
                     for t in range(T):
                         nc.vector.tensor_scalar(
                             out=tile[:, t, jj * A : (jj + 1) * A],
@@ -187,56 +198,83 @@ def tile_matchmatrix_pa_t_kernel(tc, sent_a_bytes, sent_a_scale, sent_b, W1, b1,
                         )
 
             wz_of = {}
+            hz_ps_of = {}
             hz_of = {}
+            va_of = {}
             h_of = {}
+            codes_of = {}
             x_of = {}
             yr_of = {}
             o_of = {}
 
-            def valid(g):
-                return 0 <= g < GROUPS
-
             def z_planes(g):
-                wz = work.tile([P, T, Z_J * A], F32, align_bytes=64)
-                planes(g, W_J, Z_J, wz)
-                wz_of[g] = wz
+                n, j0, size, nw, na, nz = GROUPS[g]
+                if nz:
+                    wz = work.tile([P, T, nz * A], F32, align_bytes=64, tag="wz")
+                    max_add_planes(g, nw + na, nz, wz)
+                    wz_of[g] = wz
 
-            def z_add(g, jz):
-                n = place(g)[0]
-                hz_ps = psum.tile([P, T, P], F32, tag="hz")
-                cols = slice(jz * A, (jz + 1) * A)
-                for t in range(T):
-                    nc.tensor.matmul(
-                        hz_ps[:, t, :], lhsT=wz_of[g][:, t, cols], rhs=ident[:], start=True, stop=False, is_transpose=True
-                    )
-                    nc.tensor.matmul(
-                        hz_ps[:, t, :], lhsT=t01[n][:, t, :], rhs=ident[:], start=False, stop=True, is_transpose=True
-                    )
-                return hz_ps
+            def z_add(g):
+                n, j0, size, nw, na, nz = GROUPS[g]
+                for jz in range(nz):
+                    cols = slice(jz * A, (jz + 1) * A)
+                    hz_ps = psum.tile([P, T, P], F32, tag="hz")
+                    for t in range(T):
+                        nc.tensor.matmul(
+                            hz_ps[:, t, :], lhsT=wz_of[g][:, t, cols], rhs=ident[:], start=True, stop=False, is_transpose=True
+                        )
+                        nc.tensor.matmul(
+                            hz_ps[:, t, :], lhsT=t01[n][:, t, :], rhs=ident[:], start=False, stop=True, is_transpose=True
+                        )
+                    hz_ps_of[g, jz] = hz_ps
 
-            def z_round(g, jz, hz_ps):
-                hz = work.tile([P, 2, P, 2], BF16, align_bytes=64, tag="hz", bufs=6)
-                nc.scalar.copy(out=hz[:], in_=hz_ps[:].rearrange("i (u e) m -> i u m e", e=2))
-                hz_of[g, jz] = hz
+            def z_round(g):
+                for jz in range(GROUPS[g][5]):
+                    hz = work.tile([P, 2, P, 2], BF16, align_bytes=64, tag="hz", bufs=6)
+                    nc.scalar.copy(out=hz[:], in_=hz_ps_of[g, jz][:].rearrange("i (u e) m -> i u m e", e=2))
+                    hz_of[g, jz] = hz
 
             def z_back(g):
-                wd_ps = psum.tile([P, Z_J, 2, A], F32, tag="wd")
-                for jz in range(Z_J):
-                    words = hz_of[g, jz][:].rearrange("i u m e -> i (u m e)").bitcast(F32)
-                    for u in range(2):
-                        nc.tensor.transpose(wd_ps[:, jz, u, :], words[:, u * P : (u + 1) * P], ident[:])
-                return wd_ps
+                n, j0, size, nw, na, nz = GROUPS[g]
+                if nz:
+                    wd_ps = psum.tile([P, nz, 2, A], F32, tag="wd", bufs=1)
+                    for jz in range(nz):
+                        words = hz_of[g, jz][:].rearrange("i u m e -> i (u m e)").bitcast(F32)
+                        for u in range(2):
+                            nc.tensor.transpose(wd_ps[:, jz, u, :], words[:, u * P : (u + 1) * P], ident[:])
+                    h_words = h_of[g][:, (nw + na) * A :, :].rearrange("p c t -> p (c t)").bitcast(F32)
+                    nc.scalar.copy(
+                        out=h_words.rearrange("p (j i u) -> p j i u", j=nz, u=2),
+                        in_=wd_ps[:].rearrange("p j u i -> p j i u"),
+                    )
 
-            def z_copy(g, wd_ps):
-                h_words = h_of[g][:, W_J * A :, :].rearrange("p c t -> p (c t)").bitcast(F32)
-                nc.scalar.copy(
-                    out=h_words.rearrange("p (j i u) -> p j i u", j=Z_J, u=2),
-                    in_=wd_ps[:].rearrange("p j u i -> p j i u"),
-                )
+            def a_planes(g):
+                n, j0, size, nw, na, nz = GROUPS[g]
+                if na:
+                    va = work.tile([P, T, na * A], F32, align_bytes=64, tag="va")
+                    for jj in range(na):
+                        col = slice(n * C + j0 + nw + jj, n * C + j0 + nw + jj + 1)
+                        for t in range(T):
+                            nc.scalar.activation(
+                                out=va[:, t, jj * A : (jj + 1) * A],
+                                in_=t99[n][:, t, :],
+                                func=ACT.Identity,
+                                bias=bp[t][:, col],
+                                scale=1.0 / 0.99,
+                            )
+                    va_of[g] = va
+
+            def a_leaky(g):
+                n, j0, size, nw, na, nz = GROUPS[g]
+                if na:
+                    view = va_of[g][:].rearrange("p t c -> p c t")
+                    nc.vector.scalar_tensor_tensor(
+                        out=h_of[g][:, nw * A : (nw + na) * A, :], in0=view, scalar=0.01, in1=view, op0=ALU.mult, op1=ALU.max
+                    )
 
             def w_add(g, ww):
-                n = place(g)[0]
-                for jj in range(W_J):
+                n, j0, size, nw, na, nz = GROUPS[g]
+                for jj in range(nw):
                     cols = slice(jj * A, (jj + 1) * A)
                     nc.vector.tensor_tensor(
                         out=h_of[g][:, cols, :].rearrange("p (c i) t -> p c t i", i=I4),
@@ -245,10 +283,32 @@ def tile_matchmatrix_pa_t_kernel(tc, sent_a_bytes, sent_a_scale, sent_b, W1, b1,
                         op=ALU.add,
                     )
 
+            def quantize_h(g):
+                cols = GROUPS[g][2] * A
+                h_codes = work.tile([P, cols], U32, align_bytes=64, tag="h_codes", bufs=4)
+                h_scl = work.tile([P, cols], U8, align_bytes=64, tag="h_scl", bufs=4)
+                nc.vector.quantize_mx(
+                    out=h_codes[:].bitcast(FP8X4), scales=h_scl[:], in_=h_of[g][:].rearrange("p c t -> p (c t)")
+                )
+                codes_of[g] = (h_codes, h_scl)
+
+            def multiply_h(g, x):
+                h_codes, h_scl = codes_of[g]
+                nc.tensor.matmul_mx(
+                    out=x[:],
+                    lhsT=w2_codes[:].bitcast(FP8X4),
+                    lhsT_scale=w2_scl[:],
+                    rhs=h_codes[:].bitcast(FP8X4),
+                    rhs_scale=h_scl[:],
+                    start=True,
+                    stop=True,
+                )
+
             def out_transposes(g):
                 y, r = yr_of[g]
-                o = psum.tile([P, JB, K1], F32, tag="o")
-                for jj in range(JB):
+                size = GROUPS[g][2]
+                o = psum.tile([P, size, K1], F32, tag="o")
+                for jj in range(size):
                     cols = slice(jj * A, (jj + 1) * A)
                     nc.tensor.matmul(
                         o[:, jj, :], lhsT=y[:, cols], rhs=ident[:], start=True, stop=False, is_transpose=True
@@ -258,48 +318,43 @@ def tile_matchmatrix_pa_t_kernel(tc, sent_a_bytes, sent_a_scale, sent_b, W1, b1,
                     )
                 o_of[g] = o
 
-            for g in range(-2, GROUPS + 3):
+            for g in range(-2, len(GROUPS) + 3):
                 if valid(g - 3):
-                    o_sb = work.tile([P, JB, K1], F32, align_bytes=64)
+                    n, j0, size = GROUPS[g - 3][0:3]
+                    o_sb = work.tile([P, size, K1], F32, align_bytes=64, tag="o_sb")
                     nc.scalar.copy(out=o_sb[:], in_=o_of[g - 3][:])
-                    n, j0 = place(g - 3)
-                    nc.sync.dma_start(out=out[n, :, j0 : j0 + JB, :], in_=o_sb[:])
+                    nc.sync.dma_start(out=out[n, :, j0 : j0 + size, :], in_=o_sb[:])
                 if valid(g):
-                    h = work.tile([P, COLS, T], BF16, align_bytes=64)
-                    h_of[g] = h
-                    z_copy(g, z_back(g))
+                    h_of[g] = work.tile([P, GROUPS[g][2] * A, T], BF16, align_bytes=64, tag="h", name="h")
+                    z_back(g)
+                if valid(g - 2):
+                    junk = psum.tile([P, GROUPS[g - 2][2] * A], F32, tag="junk", bufs=1)
+                    for i in range(2):
+                        multiply_h(g - 2, junk)
                 if valid(g + 2):
                     z_planes(g + 2)
                 if valid(g - 2):
-                    y = work.tile([P, COLS], F32, align_bytes=64)
+                    cols = GROUPS[g - 2][2] * A
+                    y = work.tile([P, cols], F32, align_bytes=64, tag="y")
                     nc.scalar.activation(out=y[:], in_=x_of[g - 2][:], func=ACT.Identity, bias=b2c[:])
-                    r = work.tile([P, COLS], F32, align_bytes=64)
+                    r = work.tile([P, cols], F32, align_bytes=64, tag="r")
                     nc.scalar.activation(out=r[:], in_=x_of[g - 2][:], func=ACT.Relu, bias=b2n[:], scale=-0.99)
                     yr_of[g - 2] = (y, r)
                 if valid(g + 1):
-                    z_round(g + 1, 0, z_add(g + 1, 0))
+                    z_add(g + 1)
+                    z_round(g + 1)
+                    a_planes(g + 1)
                 if valid(g - 1):
-                    h_codes = work.tile([P, COLS], U32, align_bytes=64)
-                    h_scl = work.tile([P, COLS], U8, align_bytes=64)
-                    nc.vector.quantize_mx(
-                        out=h_codes[:].bitcast(FP8X4), scales=h_scl[:], in_=h_of[g - 1][:].rearrange("p c t -> p (c t)")
-                    )
-                    x = psum.tile([P, COLS], F32, tag="x")
-                    nc.tensor.matmul_mx(
-                        out=x[:],
-                        lhsT=w2_codes[:].bitcast(FP8X4),
-                        lhsT_scale=w2_scl[:],
-                        rhs=h_codes[:].bitcast(FP8X4),
-                        rhs_scale=h_scl[:],
-                        start=True,
-                        stop=True,
-                    )
+                    quantize_h(g - 1)
+                    x = psum.tile([P, GROUPS[g - 1][2] * A], F32, tag="x")
+                    for i in range(2):
+                        multiply_h(g - 1, x)
                     x_of[g - 1] = x
-                if valid(g + 1):
-                    z_round(g + 1, 1, z_add(g + 1, 1))
                 if valid(g):
-                    ww = work.tile([P, T, W_J * A], F32, align_bytes=64)
-                    planes(g, 0, W_J, ww)
+                    nw = GROUPS[g][3]
+                    ww = work.tile([P, T, nw * A], F32, align_bytes=64, tag="ww")
+                    max_add_planes(g, 0, nw, ww)
+                    a_leaky(g)
                     w_add(g, ww)
                 if valid(g - 2):
                     out_transposes(g - 2)

@@ -18,7 +18,7 @@ ALU = mybir.AluOpType
 P = 128
 T = 4
 I4 = 4
-MIXES = {1: [(1, 0, 0)], 2: [(1, 1, 0)], 4: [(2, 1, 1), (1, 2, 1)]}
+MIXES = {1: [(1, 0, 0), (0, 1, 0)], 2: [(1, 1, 0)], 4: [(2, 1, 1), (1, 2, 1)]}
 
 
 def group_list():
@@ -67,24 +67,21 @@ def tile_matchmatrix_pa_t_kernel(tc, sent_a_bytes, sent_a_scale, sent_b, W1, b1,
         w2_codes = keep.tile([P, K1], U32, align_bytes=64)
         w2_scl = keep.tile([P, K1], U8, align_bytes=64)
         b2n = keep.tile([P, 1], F32)
-        bp = []
-        nb = []
+        bp = keep.tile([P, T, B * C], F32, align_bytes=64)
+        nb = keep.tile([P, T, B * C], F32, align_bytes=64)
         t01 = []
         t99 = []
-        for t in range(T):
-            bp.append(keep.tile([P, B * C], F32, align_bytes=64, name="bp" + str(t)))
-            nb.append(keep.tile([P, B * C], F32, align_bytes=64, name="nb" + str(t)))
         for n in range(B):
             t01.append(keep.tile([P, T, A], F32, align_bytes=64, name="t01_" + str(n)))
             t99.append(keep.tile([P, T, A], F32, align_bytes=64, name="t99_" + str(n)))
 
         with tc.manual_schedule():
+            nc.scalar.dma_start(out=a_scale[:], in_=sent_a_scale.rearrange("x y (p t) -> p (x y t)", t=T))
             nc.sync.dma_start(out=a_bytes[:], in_=sent_a_bytes.rearrange("n i k -> i n k"))
             nc.sync.dma_start(out=b_rows[:], in_=sent_b.rearrange("n j k -> (n j) k"))
             nc.sync.dma_start(out=wb_raw[:], in_=W1[D : 2 * D, :].rearrange("(p j) c -> p j c", j=T))
             nc.sync.dma_start(out=wa_raw[:], in_=W1[0:D, :].rearrange("(p j) c -> p j c", j=T))
             nc.sync.dma_start(out=w2_raw[:], in_=W2.rearrange("(p j) e -> p j e", j=T))
-            nc.scalar.dma_start(out=a_scale[:], in_=sent_a_scale.rearrange("x y (p t) -> p (x y t)", t=T))
             nc.scalar.dma_start(out=b1c[:], in_=b1.rearrange("(p t) -> p t", t=T))
             nc.scalar.dma_start(out=b2c[:], in_=b2.rearrange("(e o) -> e o", o=1))
             nc.vector.memset(warm[:], 0.0)
@@ -132,53 +129,58 @@ def tile_matchmatrix_pa_t_kernel(tc, sent_a_bytes, sent_a_scale, sent_b, W1, b1,
             for n in range(B):
                 a_ps.append(psum.tile([P, T, A], F32, tag="o", name="a_ps" + str(n)))
 
-            def bias(t):
-                nc.scalar.activation(out=bp[t][:], in_=b_ps[:, t, :], func=ACT.Identity, bias=b1c[:, t : t + 1])
-                nc.vector.tensor_scalar(out=nb[t][:], in0=bp[t][:], scalar1=-0.99, scalar2=None, op0=ALU.mult)
+            def quantized(grp, name):
+                codes = head.tile([P, P], U32, align_bytes=64, name=name + "_codes")
+                scl = head.tile([P, P], U8, align_bytes=64, name=name + "_scl")
+                nc.vector.quantize_mx(
+                    out=codes[:].bitcast(FP8X4), scales=scl[:], in_=grp[:].rearrange("p m j -> p (m j)")
+                )
+                return codes, scl
 
-            for t in range(T):
-                wb_grp = head.tile([P, P, T], BF16, align_bytes=64)
-                wa_grp = head.tile([P, P, T], BF16, align_bytes=64)
-                nc.scalar.copy(out=wb_grp[:], in_=wb_raw[:].rearrange("p j (m t) -> p t m j", t=T)[:, t])
-                nc.vector.tensor_copy(out=wa_grp[:], in_=wa_raw[:].rearrange("p j (m t) -> p t m j", t=T)[:, t])
-                wb_codes = head.tile([P, P], U32, align_bytes=64)
-                wb_scl = head.tile([P, P], U8, align_bytes=64)
-                wa_codes = head.tile([P, P], U32, align_bytes=64)
-                wa_scl = head.tile([P, P], U8, align_bytes=64)
-                nc.vector.quantize_mx(
-                    out=wb_codes[:].bitcast(FP8X4), scales=wb_scl[:], in_=wb_grp[:].rearrange("p m j -> p (m j)")
-                )
-                nc.vector.quantize_mx(
-                    out=wa_codes[:].bitcast(FP8X4), scales=wa_scl[:], in_=wa_grp[:].rearrange("p m j -> p (m j)")
-                )
+            def head_matmul(out_ap, weights, codes_ap, scl_ap):
                 nc.tensor.matmul_mx(
-                    out=b_ps[:, t, :],
-                    lhsT=wb_codes[:].bitcast(FP8X4),
-                    lhsT_scale=wb_scl[:],
-                    rhs=b_codes[:].bitcast(FP8X4),
-                    rhs_scale=b_scl[:],
+                    out=out_ap,
+                    lhsT=weights[0][:].bitcast(FP8X4),
+                    lhsT_scale=weights[1][:],
+                    rhs=codes_ap.bitcast(FP8X4),
+                    rhs_scale=scl_ap,
                     start=True,
                     stop=True,
                 )
-                for n in range(B):
-                    nc.tensor.matmul_mx(
-                        out=a_ps[n][:, t, :],
-                        lhsT=wa_codes[:].bitcast(FP8X4),
-                        lhsT_scale=wa_scl[:],
-                        rhs=a_codes[:, n * A : (n + 1) * A].bitcast(FP8X4),
-                        rhs_scale=a_scl[:, n * A : (n + 1) * A],
-                        start=True,
-                        stop=True,
-                    )
+
+            def a_matmul(n, t):
+                cols = slice(n * A, (n + 1) * A)
+                head_matmul(a_ps[n][:, t, :], wa_of[t], a_codes[:, cols], a_scl[:, cols])
+
+            wb_grps = []
             for t in range(T):
-                bias(t)
-            for n in range(B):
-                nc.scalar.activation(out=t99[n][:], in_=a_ps[n][:], func=ACT.Copy, scale=0.99)
-                nc.scalar.activation(out=t01[n][:], in_=a_ps[n][:], func=ACT.Copy, scale=0.01)
-            nc.vector.tensor_copy(out=w2_grp[:], in_=w2_raw[:].rearrange("p j e -> p e j"))
-            nc.vector.quantize_mx(
-                out=w2_codes[:].bitcast(FP8X4), scales=w2_scl[:], in_=w2_grp[:].rearrange("p e j -> p (e j)")
-            )
+                wb_grp = head.tile([P, P, T], BF16, align_bytes=64)
+                nc.scalar.copy(out=wb_grp[:], in_=wb_raw[:].rearrange("p j (m t) -> p t m j", t=T)[:, t])
+                wb_grps.append(wb_grp)
+            wa_grps = []
+            for t in range(T):
+                wa_grp = head.tile([P, P, T], BF16, align_bytes=64)
+                if t < T - 1:
+                    nc.vector.tensor_copy(out=wa_grp[:], in_=wa_raw[:].rearrange("p j (m t) -> p t m j", t=T)[:, t])
+                else:
+                    nc.scalar.copy(out=wa_grp[:], in_=wa_raw[:].rearrange("p j (m t) -> p t m j", t=T)[:, t])
+                wa_grps.append(wa_grp)
+                wb_q = quantized(wb_grps[t], "wb")
+                head_matmul(b_ps[:, t, :], wb_q, b_codes[:], b_scl[:])
+            wa_of = []
+            for t in range(T):
+                wa_of.append(quantized(wa_grps[t], "wa"))
+                a_matmul(0, t)
+            for t in range(T):
+                nc.vector.tensor_scalar(
+                    out=bp[:, t, :], in0=b_ps[:, t, :], scalar1=b1c[:, t : t + 1], scalar2=None, op0=ALU.add
+                )
+                nc.scalar.activation(out=t99[0][:, t, :], in_=a_ps[0][:, t, :], func=ACT.Copy, scale=0.99)
+            nc.scalar.copy(out=w2_grp[:], in_=w2_raw[:].rearrange("p j e -> p e j"))
+            for t in range(T):
+                a_matmul(1, t)
+            nc.vector.tensor_scalar(out=nb[:], in0=bp[:], scalar1=-0.99, scalar2=None, op0=ALU.mult)
+            nc.scalar.activation(out=t01[0][:], in_=a_ps[0][:], func=ACT.Copy, scale=0.01)
 
             def valid(g):
                 return 0 <= g < len(GROUPS)
@@ -191,8 +193,8 @@ def tile_matchmatrix_pa_t_kernel(tc, sent_a_bytes, sent_a_scale, sent_b, W1, b1,
                         nc.vector.tensor_scalar(
                             out=tile[:, t, jj * A : (jj + 1) * A],
                             in0=t99[n][:, t, :],
-                            scalar1=nb[t][:, col],
-                            scalar2=bp[t][:, col],
+                            scalar1=nb[:, t, col],
+                            scalar2=bp[:, t, col],
                             op0=ALU.max,
                             op1=ALU.add,
                         )
@@ -200,6 +202,7 @@ def tile_matchmatrix_pa_t_kernel(tc, sent_a_bytes, sent_a_scale, sent_b, W1, b1,
             wz_of = {}
             hz_ps_of = {}
             hz_of = {}
+            wd_of = {}
             va_of = {}
             h_of = {}
             codes_of = {}
@@ -242,10 +245,15 @@ def tile_matchmatrix_pa_t_kernel(tc, sent_a_bytes, sent_a_scale, sent_b, W1, b1,
                         words = hz_of[g, jz][:].rearrange("i u m e -> i (u m e)").bitcast(F32)
                         for u in range(2):
                             nc.tensor.transpose(wd_ps[:, jz, u, :], words[:, u * P : (u + 1) * P], ident[:])
+                    wd_of[g] = wd_ps
+
+            def z_copy(g):
+                n, j0, size, nw, na, nz = GROUPS[g]
+                if nz:
                     h_words = h_of[g][:, (nw + na) * A :, :].rearrange("p c t -> p (c t)").bitcast(F32)
                     nc.scalar.copy(
                         out=h_words.rearrange("p (j i u) -> p j i u", j=nz, u=2),
-                        in_=wd_ps[:].rearrange("p j u i -> p j i u"),
+                        in_=wd_of[g][:].rearrange("p j u i -> p j i u"),
                     )
 
             def a_planes(g):
@@ -259,7 +267,7 @@ def tile_matchmatrix_pa_t_kernel(tc, sent_a_bytes, sent_a_scale, sent_b, W1, b1,
                                 out=va[:, t, jj * A : (jj + 1) * A],
                                 in_=t99[n][:, t, :],
                                 func=ACT.Identity,
-                                bias=bp[t][:, col],
+                                bias=bp[:, t, col],
                                 scale=1.0 / 0.99,
                             )
                     va_of[g] = va
@@ -318,19 +326,11 @@ def tile_matchmatrix_pa_t_kernel(tc, sent_a_bytes, sent_a_scale, sent_b, W1, b1,
                     )
                 o_of[g] = o
 
+            last = len(GROUPS) - 1
             for g in range(-2, len(GROUPS) + 3):
-                if valid(g - 3):
-                    n, j0, size = GROUPS[g - 3][0:3]
-                    o_sb = work.tile([P, size, K1], F32, align_bytes=64, tag="o_sb")
-                    nc.scalar.copy(out=o_sb[:], in_=o_of[g - 3][:])
-                    nc.sync.dma_start(out=out[n, :, j0 : j0 + size, :], in_=o_sb[:])
                 if valid(g):
                     h_of[g] = work.tile([P, GROUPS[g][2] * A, T], BF16, align_bytes=64, tag="h", name="h")
                     z_back(g)
-                if valid(g - 2):
-                    junk = psum.tile([P, GROUPS[g - 2][2] * A], F32, tag="junk", bufs=1)
-                    for i in range(2):
-                        multiply_h(g - 2, junk)
                 if valid(g + 2):
                     z_planes(g + 2)
                 if valid(g - 2):
@@ -338,23 +338,47 @@ def tile_matchmatrix_pa_t_kernel(tc, sent_a_bytes, sent_a_scale, sent_b, W1, b1,
                     y = work.tile([P, cols], F32, align_bytes=64, tag="y")
                     nc.scalar.activation(out=y[:], in_=x_of[g - 2][:], func=ACT.Identity, bias=b2c[:])
                     r = work.tile([P, cols], F32, align_bytes=64, tag="r")
-                    nc.scalar.activation(out=r[:], in_=x_of[g - 2][:], func=ACT.Relu, bias=b2n[:], scale=-0.99)
+                    if g - 2 >= last - 1:
+                        nc.vector.tensor_scalar(
+                            out=r[:], in0=y[:], scalar1=0.0, scalar2=-0.99, op0=ALU.min, op1=ALU.mult
+                        )
+                    else:
+                        nc.scalar.activation(out=r[:], in_=x_of[g - 2][:], func=ACT.Relu, bias=b2n[:], scale=-0.99)
                     yr_of[g - 2] = (y, r)
+                if valid(g - 3):
+                    n, j0, size = GROUPS[g - 3][0:3]
+                    o_sb = work.tile([P, size, K1], F32, align_bytes=64, tag="o_sb")
+                    nc.scalar.copy(out=o_sb[:], in_=o_of[g - 3][:])
+                    nc.sync.dma_start(out=out[n, :, j0 : j0 + size, :], in_=o_sb[:])
+                if valid(g):
+                    z_copy(g)
                 if valid(g + 1):
                     z_add(g + 1)
                     z_round(g + 1)
                     a_planes(g + 1)
+                if g == 1:
+                    nc.scalar.activation(out=t99[1][:], in_=a_ps[1][:], func=ACT.Copy, scale=0.99)
+                    nc.scalar.activation(out=t01[1][:], in_=a_ps[1][:], func=ACT.Copy, scale=0.01)
                 if valid(g - 1):
                     quantize_h(g - 1)
                     x = psum.tile([P, GROUPS[g - 1][2] * A], F32, tag="x")
-                    for i in range(2):
+                    for i in range(1):
                         multiply_h(g - 1, x)
                     x_of[g - 1] = x
                 if valid(g):
                     nw = GROUPS[g][3]
-                    ww = work.tile([P, T, nw * A], F32, align_bytes=64, tag="ww")
-                    max_add_planes(g, 0, nw, ww)
+                    if nw:
+                        ww = work.tile([P, T, nw * A], F32, align_bytes=64, tag="ww")
+                        max_add_planes(g, 0, nw, ww)
+                    if g == 0:
+                        nc.vector.quantize_mx(
+                            out=w2_codes[:].bitcast(FP8X4), scales=w2_scl[:], in_=w2_grp[:].rearrange("p e j -> p (e j)")
+                        )
                     a_leaky(g)
                     w_add(g, ww)
                 if valid(g - 2):
                     out_transposes(g - 2)
+                    if False:
+                        junk = psum.tile([P, GROUPS[g - 2][2] * A], F32, tag="junk", bufs=1)
+                        for i in range(2):
+                            multiply_h(g - 2, junk)

@@ -5,6 +5,7 @@ from concourse.masks import make_identity
 
 B, A, C, D, K0, K1 = 2, 128, 64, 512, 512, 128
 FLOPS = 2 * B * A * C * K0 * K1 + 2 * B * A * D * K0 + 2 * B * C * D * K0
+SLOPE = 0.01
 
 F32 = mybir.dt.float32
 BF16 = mybir.dt.bfloat16
@@ -17,31 +18,36 @@ ALU = mybir.AluOpType
 
 P = 128
 T = 4
-I4 = 4
-MIXES = {1: [(1, 0, 0), (0, 1, 0)], 2: [(1, 1, 0)], 4: [(2, 1, 1), (1, 2, 1)]}
+RUN = 4
+PLANE_GAP = 4
+
+MIXTURES = {
+    1: [(1, 0, 0), (0, 1, 0)],
+    2: [(1, 1, 0)],
+    4: [(2, 1, 1), (1, 2, 1)],
+}
+SIZES = {0: [1, 1, 2] + [4] * 15, 1: [4] * 15 + [2, 1, 1]}
 
 
 def group_list():
     groups = []
     for n in range(B):
-        sizes = [4] * 15
-        sizes = [1, 1, 2] + sizes if n == 0 else sizes + [2, 1, 1]
         j = 0
-        for i, size in enumerate(sizes):
-            mixes = MIXES[size]
-            groups.append((n, j, size) + mixes[i % len(mixes)])
+        for i, size in enumerate(SIZES[n]):
+            mixtures = MIXTURES[size]
+            groups.append((n, j, size) + mixtures[i % len(mixtures)])
             j += size
     return groups
 
 
-GROUPS = group_list()
-
-
 def tile_matchmatrix_pa_t_kernel(tc, sent_a_bytes, sent_a_scale, sent_b, W1, b1, W2, b2, out):
     nc = tc.nc
+    groups = group_list()
+    last = len(groups) - 1
+
     with ExitStack() as ctx:
         keep = ctx.enter_context(tc.tile_pool(name="keep", bufs=1))
-        head = ctx.enter_context(tc.tile_pool(name="head", bufs=4))
+        head = ctx.enter_context(tc.tile_pool(name="head", bufs=T))
         work = ctx.enter_context(tc.tile_pool(name="work", bufs=3))
         psum = ctx.enter_context(tc.psum_pool(name="psum", bufs=2))
 
@@ -51,53 +57,68 @@ def tile_matchmatrix_pa_t_kernel(tc, sent_a_bytes, sent_a_scale, sent_b, W1, b1,
         wb_raw = keep.tile([P, T, K0], BF16, align_bytes=64)
         wa_raw = keep.tile([P, T, K0], BF16, align_bytes=64)
         w2_raw = keep.tile([P, T, K1], BF16, align_bytes=64)
-        b1c = keep.tile([P, T], BF16)
-        b2c = keep.tile([P, 1], BF16)
+        b1_cols = keep.tile([P, T], BF16)
+        b2_col = keep.tile([P, 1], BF16)
+        neg_b2 = keep.tile([P, 1], F32)
         ident = keep.tile([P, P], F32, align_bytes=64)
-        warm = keep.tile([P, 1], F32)
+        dummy = keep.tile([P, 1], F32)
 
         a_wide = keep.tile([P, B, D], BF16, align_bytes=64)
         a_grp = keep.tile([P, B, A, T], BF16, align_bytes=64)
         b_grp = keep.tile([P, P, T], BF16, align_bytes=64)
+        w2_grp = keep.tile([P, K1, T], BF16, align_bytes=64)
         a_codes = keep.tile([P, B * A], U32, align_bytes=64)
         a_scl = keep.tile([P, B * A], U8, align_bytes=64)
         b_codes = keep.tile([P, P], U32, align_bytes=64)
         b_scl = keep.tile([P, P], U8, align_bytes=64)
-        w2_grp = keep.tile([P, K1, T], BF16, align_bytes=64)
         w2_codes = keep.tile([P, K1], U32, align_bytes=64)
         w2_scl = keep.tile([P, K1], U8, align_bytes=64)
-        b2n = keep.tile([P, 1], F32)
-        bp = keep.tile([P, T, B * C], F32, align_bytes=64)
-        nb = keep.tile([P, T, B * C], F32, align_bytes=64)
-        t01 = []
-        t99 = []
+
+        b_plus = keep.tile([P, T, B * C], F32, align_bytes=64)
+        b_neg = keep.tile([P, T, B * C], F32, align_bytes=64)
+        a_low = []
+        a_high = []
         for n in range(B):
-            t01.append(keep.tile([P, T, A], F32, align_bytes=64, name="t01_" + str(n)))
-            t99.append(keep.tile([P, T, A], F32, align_bytes=64, name="t99_" + str(n)))
+            a_low.append(keep.tile([P, T, A], F32, align_bytes=64, name="a_low" + str(n)))
+            a_high.append(keep.tile([P, T, A], F32, align_bytes=64, name="a_high" + str(n)))
+
+        def quantize(codes, scl, grouped):
+            nc.vector.quantize_mx(
+                out=codes[:].bitcast(FP8X4), scales=scl[:], in_=grouped[:].rearrange("p c t -> p (c t)")
+            )
+
+        def multiply(out_ap, weights, rhs_codes, rhs_scl):
+            nc.tensor.matmul_mx(
+                out=out_ap,
+                lhsT=weights[0][:].bitcast(FP8X4),
+                lhsT_scale=weights[1][:],
+                rhs=rhs_codes.bitcast(FP8X4),
+                rhs_scale=rhs_scl,
+                start=True,
+                stop=True,
+            )
+
+        def transpose_sum(out_ap, first, second):
+            nc.tensor.matmul(out_ap, lhsT=first, rhs=ident[:], start=True, stop=False, is_transpose=True)
+            nc.tensor.matmul(out_ap, lhsT=second, rhs=ident[:], start=False, stop=True, is_transpose=True)
 
         with tc.manual_schedule():
             nc.scalar.dma_start(out=a_scale[:], in_=sent_a_scale.rearrange("x y (p t) -> p (x y t)", t=T))
             nc.sync.dma_start(out=a_bytes[:], in_=sent_a_bytes.rearrange("n i k -> i n k"))
             nc.sync.dma_start(out=b_rows[:], in_=sent_b.rearrange("n j k -> (n j) k"))
-            nc.sync.dma_start(out=wb_raw[:], in_=W1[D : 2 * D, :].rearrange("(p j) c -> p j c", j=T))
-            nc.sync.dma_start(out=wa_raw[:], in_=W1[0:D, :].rearrange("(p j) c -> p j c", j=T))
-            nc.sync.dma_start(out=w2_raw[:], in_=W2.rearrange("(p j) e -> p j e", j=T))
-            nc.scalar.dma_start(out=b1c[:], in_=b1.rearrange("(p t) -> p t", t=T))
-            nc.scalar.dma_start(out=b2c[:], in_=b2.rearrange("(e o) -> e o", o=1))
-            nc.vector.memset(warm[:], 0.0)
-            nc.scalar.activation(out=warm[:], in_=warm[:], func=ACT.Identity)
+            nc.sync.dma_start(out=wb_raw[:], in_=W1[D : 2 * D, :].rearrange("(p t) c -> p t c", t=T))
+            nc.sync.dma_start(out=wa_raw[:], in_=W1[0:D, :].rearrange("(p t) c -> p t c", t=T))
+            nc.sync.dma_start(out=w2_raw[:], in_=W2.rearrange("(p t) e -> p t e", t=T))
+            nc.scalar.dma_start(out=b1_cols[:], in_=b1.rearrange("(p t) -> p t", t=T))
+            nc.scalar.dma_start(out=b2_col[:], in_=b2.rearrange("(e o) -> e o", o=1))
+            nc.vector.memset(dummy[:], 0.0)
+            nc.scalar.activation(out=dummy[:], in_=dummy[:], func=ACT.Identity)
             make_identity(nc, ident[:])
-
-            def widen(n, engine):
-                if engine == "v":
-                    nc.vector.tensor_copy(out=a_wide[:, n, :], in_=a_bytes[:, n, :].bitcast(FP8))
-                else:
-                    nc.scalar.activation(out=a_wide[:, n, :], in_=a_bytes[:, n, :].bitcast(FP8), func=ACT.Copy)
 
             at_ps = psum.tile([P, B, 2, A], F32, tag="hz")
             bt_ps = psum.tile([P, 2, P], F32, tag="hz")
-            widen(0, "v")
-            widen(1, "s")
+            nc.vector.tensor_copy(out=a_wide[:, 0, :], in_=a_bytes[:, 0, :].bitcast(FP8))
+            nc.scalar.activation(out=a_wide[:, 1, :], in_=a_bytes[:, 1, :].bitcast(FP8), func=ACT.Copy)
             a_words = a_wide[:].bitcast(F32)
             b_words = b_rows[:].bitcast(F32)
             for u in range(2):
@@ -116,269 +137,215 @@ def tile_matchmatrix_pa_t_kernel(tc, sent_a_bytes, sent_a_scale, sent_b, W1, b1,
                     in1=a_scale[:].rearrange("p (u e) -> p u e", u=2).unsqueeze(1).to_broadcast([P, A, 2, 2]),
                     op=ALU.mult,
                 )
-            nc.vector.quantize_mx(
-                out=b_codes[:].bitcast(FP8X4), scales=b_scl[:], in_=b_grp[:].rearrange("p r t -> p (r t)")
-            )
+            quantize(b_codes, b_scl, b_grp)
             nc.vector.quantize_mx(
                 out=a_codes[:].bitcast(FP8X4), scales=a_scl[:], in_=a_grp[:].rearrange("p n i t -> p (n i t)")
             )
+            nc.vector.tensor_scalar(out=neg_b2[:], in0=b2_col[:], scalar1=SLOPE - 1.0, scalar2=None, op0=ALU.mult)
 
-            nc.vector.tensor_scalar(out=b2n[:], in0=b2c[:], scalar1=-0.99, scalar2=None, op0=ALU.mult)
             b_ps = psum.tile([P, T, B * C], F32, tag="x")
             a_ps = []
             for n in range(B):
                 a_ps.append(psum.tile([P, T, A], F32, tag="o", name="a_ps" + str(n)))
 
-            def quantized(grp, name):
+            def weight_chunk(copy, raw, t, name):
+                grouped = head.tile([P, P, T], BF16, align_bytes=64, name=name)
+                copy(out=grouped[:], in_=raw[:].rearrange("p j (m t) -> p t m j", t=T)[:, t])
+                return grouped
+
+            def quantized_chunk(grouped, name):
                 codes = head.tile([P, P], U32, align_bytes=64, name=name + "_codes")
                 scl = head.tile([P, P], U8, align_bytes=64, name=name + "_scl")
-                nc.vector.quantize_mx(
-                    out=codes[:].bitcast(FP8X4), scales=scl[:], in_=grp[:].rearrange("p m j -> p (m j)")
-                )
+                quantize(codes, scl, grouped)
                 return codes, scl
 
-            def head_matmul(out_ap, weights, codes_ap, scl_ap):
-                nc.tensor.matmul_mx(
-                    out=out_ap,
-                    lhsT=weights[0][:].bitcast(FP8X4),
-                    lhsT_scale=weights[1][:],
-                    rhs=codes_ap.bitcast(FP8X4),
-                    rhs_scale=scl_ap,
-                    start=True,
-                    stop=True,
-                )
-
-            def a_matmul(n, t):
+            def a_multiply(n, t):
                 cols = slice(n * A, (n + 1) * A)
-                head_matmul(a_ps[n][:, t, :], wa_of[t], a_codes[:, cols], a_scl[:, cols])
+                multiply(a_ps[n][:, t, :], wa_chunks[t], a_codes[:, cols], a_scl[:, cols])
 
             wb_grps = []
             for t in range(T):
-                wb_grp = head.tile([P, P, T], BF16, align_bytes=64)
-                nc.scalar.copy(out=wb_grp[:], in_=wb_raw[:].rearrange("p j (m t) -> p t m j", t=T)[:, t])
-                wb_grps.append(wb_grp)
+                wb_grps.append(weight_chunk(nc.scalar.copy, wb_raw, t, "wb_grp"))
             wa_grps = []
             for t in range(T):
-                wa_grp = head.tile([P, P, T], BF16, align_bytes=64)
-                if t < T - 1:
-                    nc.vector.tensor_copy(out=wa_grp[:], in_=wa_raw[:].rearrange("p j (m t) -> p t m j", t=T)[:, t])
-                else:
-                    nc.scalar.copy(out=wa_grp[:], in_=wa_raw[:].rearrange("p j (m t) -> p t m j", t=T)[:, t])
-                wa_grps.append(wa_grp)
-                wb_q = quantized(wb_grps[t], "wb")
-                head_matmul(b_ps[:, t, :], wb_q, b_codes[:], b_scl[:])
-            wa_of = []
+                copy = nc.scalar.copy if t == T - 1 else nc.vector.tensor_copy
+                wa_grps.append(weight_chunk(copy, wa_raw, t, "wa_grp"))
+                multiply(b_ps[:, t, :], quantized_chunk(wb_grps[t], "wb"), b_codes[:], b_scl[:])
+            wa_chunks = []
             for t in range(T):
-                wa_of.append(quantized(wa_grps[t], "wa"))
-                a_matmul(0, t)
+                wa_chunks.append(quantized_chunk(wa_grps[t], "wa"))
+                a_multiply(0, t)
             for t in range(T):
                 nc.vector.tensor_scalar(
-                    out=bp[:, t, :], in0=b_ps[:, t, :], scalar1=b1c[:, t : t + 1], scalar2=None, op0=ALU.add
+                    out=b_plus[:, t, :], in0=b_ps[:, t, :], scalar1=b1_cols[:, t : t + 1], scalar2=None, op0=ALU.add
                 )
-                nc.scalar.activation(out=t99[0][:, t, :], in_=a_ps[0][:, t, :], func=ACT.Copy, scale=0.99)
-            nc.scalar.copy(out=w2_grp[:], in_=w2_raw[:].rearrange("p j e -> p e j"))
+                nc.scalar.activation(out=a_high[0][:, t, :], in_=a_ps[0][:, t, :], func=ACT.Copy, scale=1.0 - SLOPE)
             for t in range(T):
-                a_matmul(1, t)
-            nc.vector.tensor_scalar(out=nb[:], in0=bp[:], scalar1=-0.99, scalar2=None, op0=ALU.mult)
-            nc.scalar.activation(out=t01[0][:], in_=a_ps[0][:], func=ACT.Copy, scale=0.01)
+                a_multiply(1, t)
+            nc.vector.tensor_scalar(out=b_neg[:], in0=b_plus[:], scalar1=SLOPE - 1.0, scalar2=None, op0=ALU.mult)
+            nc.scalar.activation(out=a_low[0][:], in_=a_ps[0][:], func=ACT.Copy, scale=SLOPE)
+            nc.scalar.copy(out=w2_grp[:], in_=w2_raw[:].rearrange("p t e -> p e t"))
+
+            z_planes_of, z_sum_of, z_rows_of, z_words_of, s_planes_of = {}, {}, {}, {}, {}
+            h_of, x_of, y_of, out_of = {}, {}, {}, {}
 
             def valid(g):
-                return 0 <= g < len(GROUPS)
+                return 0 <= g <= last
 
-            def max_add_planes(g, first, count, tile):
-                n, j0 = GROUPS[g][0:2]
+            def w_planes(g, first, count, tag):
+                n, j0 = groups[g][0:2]
+                planes = work.tile([P, T, count * A], F32, align_bytes=64, tag=tag, name=tag)
                 for jj in range(count):
                     col = slice(n * C + j0 + first + jj, n * C + j0 + first + jj + 1)
                     for t in range(T):
                         nc.vector.tensor_scalar(
-                            out=tile[:, t, jj * A : (jj + 1) * A],
-                            in0=t99[n][:, t, :],
-                            scalar1=nb[:, t, col],
-                            scalar2=bp[:, t, col],
+                            out=planes[:, t, jj * A : (jj + 1) * A],
+                            in0=a_high[n][:, t, :],
+                            scalar1=b_neg[:, t, col],
+                            scalar2=b_plus[:, t, col],
                             op0=ALU.max,
                             op1=ALU.add,
                         )
+                return planes
 
-            wz_of = {}
-            hz_ps_of = {}
-            hz_of = {}
-            wd_of = {}
-            va_of = {}
-            h_of = {}
-            codes_of = {}
-            x_of = {}
-            yr_of = {}
-            o_of = {}
-
-            def z_planes(g):
-                n, j0, size, nw, na, nz = GROUPS[g]
-                if nz:
-                    wz = work.tile([P, T, nz * A], F32, align_bytes=64, tag="wz")
-                    max_add_planes(g, nw + na, nz, wz)
-                    wz_of[g] = wz
-
-            def z_add(g):
-                n, j0, size, nw, na, nz = GROUPS[g]
-                for jz in range(nz):
-                    cols = slice(jz * A, (jz + 1) * A)
-                    hz_ps = psum.tile([P, T, P], F32, tag="hz")
-                    for t in range(T):
-                        nc.tensor.matmul(
-                            hz_ps[:, t, :], lhsT=wz_of[g][:, t, cols], rhs=ident[:], start=True, stop=False, is_transpose=True
-                        )
-                        nc.tensor.matmul(
-                            hz_ps[:, t, :], lhsT=t01[n][:, t, :], rhs=ident[:], start=False, stop=True, is_transpose=True
-                        )
-                    hz_ps_of[g, jz] = hz_ps
-
-            def z_round(g):
-                for jz in range(GROUPS[g][5]):
-                    hz = work.tile([P, 2, P, 2], BF16, align_bytes=64, tag="hz", bufs=6)
-                    nc.scalar.copy(out=hz[:], in_=hz_ps_of[g, jz][:].rearrange("i (u e) m -> i u m e", e=2))
-                    hz_of[g, jz] = hz
-
-            def z_back(g):
-                n, j0, size, nw, na, nz = GROUPS[g]
-                if nz:
-                    wd_ps = psum.tile([P, nz, 2, A], F32, tag="wd", bufs=1)
-                    for jz in range(nz):
-                        words = hz_of[g, jz][:].rearrange("i u m e -> i (u m e)").bitcast(F32)
-                        for u in range(2):
-                            nc.tensor.transpose(wd_ps[:, jz, u, :], words[:, u * P : (u + 1) * P], ident[:])
-                    wd_of[g] = wd_ps
-
-            def z_copy(g):
-                n, j0, size, nw, na, nz = GROUPS[g]
-                if nz:
-                    h_words = h_of[g][:, (nw + na) * A :, :].rearrange("p c t -> p (c t)").bitcast(F32)
-                    nc.scalar.copy(
-                        out=h_words.rearrange("p (j i u) -> p j i u", j=nz, u=2),
-                        in_=wd_of[g][:].rearrange("p j u i -> p j i u"),
-                    )
-
-            def a_planes(g):
-                n, j0, size, nw, na, nz = GROUPS[g]
-                if na:
-                    va = work.tile([P, T, na * A], F32, align_bytes=64, tag="va")
-                    for jj in range(na):
-                        col = slice(n * C + j0 + nw + jj, n * C + j0 + nw + jj + 1)
-                        for t in range(T):
-                            nc.scalar.activation(
-                                out=va[:, t, jj * A : (jj + 1) * A],
-                                in_=t99[n][:, t, :],
-                                func=ACT.Identity,
-                                bias=bp[:, t, col],
-                                scale=1.0 / 0.99,
-                            )
-                    va_of[g] = va
-
-            def a_leaky(g):
-                n, j0, size, nw, na, nz = GROUPS[g]
-                if na:
-                    view = va_of[g][:].rearrange("p t c -> p c t")
-                    nc.vector.scalar_tensor_tensor(
-                        out=h_of[g][:, nw * A : (nw + na) * A, :], in0=view, scalar=0.01, in1=view, op0=ALU.mult, op1=ALU.max
-                    )
-
-            def w_add(g, ww):
-                n, j0, size, nw, na, nz = GROUPS[g]
+            def w_sum(g, planes):
+                n, nw = groups[g][0], groups[g][3]
                 for jj in range(nw):
                     cols = slice(jj * A, (jj + 1) * A)
                     nc.vector.tensor_tensor(
-                        out=h_of[g][:, cols, :].rearrange("p (c i) t -> p c t i", i=I4),
-                        in0=t01[n][:].rearrange("p t (c i) -> p c t i", i=I4),
-                        in1=ww[:, :, cols].rearrange("p t (c i) -> p c t i", i=I4),
+                        out=h_of[g][:, cols, :].rearrange("p (c i) t -> p c t i", i=RUN),
+                        in0=a_low[n][:].rearrange("p t (c i) -> p c t i", i=RUN),
+                        in1=planes[:, :, cols].rearrange("p t (c i) -> p c t i", i=RUN),
                         op=ALU.add,
                     )
 
-            def quantize_h(g):
-                cols = GROUPS[g][2] * A
-                h_codes = work.tile([P, cols], U32, align_bytes=64, tag="h_codes", bufs=4)
-                h_scl = work.tile([P, cols], U8, align_bytes=64, tag="h_scl", bufs=4)
-                nc.vector.quantize_mx(
-                    out=h_codes[:].bitcast(FP8X4), scales=h_scl[:], in_=h_of[g][:].rearrange("p c t -> p (c t)")
-                )
-                codes_of[g] = (h_codes, h_scl)
+            def s_planes(g):
+                n, j0, size, nw, ns, nz = groups[g]
+                if ns:
+                    planes = work.tile([P, T, ns * A + PLANE_GAP], F32, align_bytes=64, tag="s_planes")
+                    for jj in range(ns):
+                        col = slice(n * C + j0 + nw + jj, n * C + j0 + nw + jj + 1)
+                        for t in range(T):
+                            nc.scalar.activation(
+                                out=planes[:, t, jj * A : (jj + 1) * A],
+                                in_=a_high[n][:, t, :],
+                                func=ACT.Identity,
+                                bias=b_plus[:, t, col],
+                                scale=1.0 / (1.0 - SLOPE),
+                            )
+                    s_planes_of[g] = planes
 
-            def multiply_h(g, x):
-                h_codes, h_scl = codes_of[g]
-                nc.tensor.matmul_mx(
-                    out=x[:],
-                    lhsT=w2_codes[:].bitcast(FP8X4),
-                    lhsT_scale=w2_scl[:],
-                    rhs=h_codes[:].bitcast(FP8X4),
-                    rhs_scale=h_scl[:],
-                    start=True,
-                    stop=True,
-                )
+            def s_leaky(g):
+                n, j0, size, nw, ns, nz = groups[g]
+                if ns:
+                    v = s_planes_of[g][:, :, 0 : ns * A].rearrange("p t c -> p c t")
+                    nc.vector.scalar_tensor_tensor(
+                        out=h_of[g][:, nw * A : (nw + ns) * A, :], in0=v, scalar=SLOPE, in1=v, op0=ALU.mult, op1=ALU.max
+                    )
 
-            def out_transposes(g):
-                y, r = yr_of[g]
-                size = GROUPS[g][2]
-                o = psum.tile([P, size, K1], F32, tag="o")
+            def z_sums(g):
+                n, nz = groups[g][0], groups[g][5]
+                for jz in range(nz):
+                    z_sum = psum.tile([P, T, P], F32, tag="hz")
+                    for t in range(T):
+                        w = z_planes_of[g][:, t, jz * A : (jz + 1) * A]
+                        transpose_sum(z_sum[:, t, :], w, a_low[n][:, t, :])
+                    z_sum_of[g, jz] = z_sum
+
+            def z_round(g):
+                for jz in range(groups[g][5]):
+                    rows = work.tile([P, 2, P, 2], BF16, align_bytes=64, tag="z_rows")
+                    nc.scalar.copy(out=rows[:], in_=z_sum_of[g, jz][:].rearrange("i (u e) m -> i u m e", e=2))
+                    z_rows_of[g, jz] = rows
+
+            def z_back(g):
+                nz = groups[g][5]
+                if nz:
+                    words = psum.tile([P, nz, 2, A], F32, tag="words", bufs=1)
+                    for jz in range(nz):
+                        rows = z_rows_of[g, jz][:].rearrange("i u m e -> i (u m e)").bitcast(F32)
+                        for u in range(2):
+                            nc.tensor.transpose(words[:, jz, u, :], rows[:, u * P : (u + 1) * P], ident[:])
+                    z_words_of[g] = words
+
+            def z_copy(g):
+                n, j0, size, nw, ns, nz = groups[g]
+                if nz:
+                    h_words = h_of[g][:, (nw + ns) * A :, :].rearrange("p c t -> p (c t)").bitcast(F32)
+                    nc.scalar.copy(
+                        out=h_words.rearrange("p (j i u) -> p j i u", j=nz, u=2),
+                        in_=z_words_of[g][:].rearrange("p j u i -> p j i u"),
+                    )
+
+            def second_layer(g):
+                cols = groups[g][2] * A
+                h_codes = work.tile([P, cols], U32, align_bytes=64, tag="h_codes")
+                h_scl = work.tile([P, cols], U8, align_bytes=64, tag="h_scl")
+                quantize(h_codes, h_scl, h_of[g])
+                x = psum.tile([P, cols], F32, tag="x")
+                multiply(x[:], (w2_codes, w2_scl), h_codes[:], h_scl[:])
+                x_of[g] = x
+
+            def bias_and_rest(g):
+                cols = groups[g][2] * A
+                y = work.tile([P, cols], F32, align_bytes=64, tag="y")
+                nc.scalar.activation(out=y[:], in_=x_of[g][:], func=ACT.Identity, bias=b2_col[:])
+                rest = work.tile([P, cols], F32, align_bytes=64, tag="rest")
+                if g >= last - 1:
+                    nc.vector.tensor_scalar(
+                        out=rest[:], in0=y[:], scalar1=0.0, scalar2=SLOPE - 1.0, op0=ALU.min, op1=ALU.mult
+                    )
+                else:
+                    nc.scalar.activation(
+                        out=rest[:], in_=x_of[g][:], func=ACT.Relu, bias=neg_b2[:], scale=SLOPE - 1.0
+                    )
+                y_of[g] = (y, rest)
+
+            def turn_output(g):
+                y, rest = y_of[g]
+                size = groups[g][2]
+                turned = psum.tile([P, size, K1], F32, tag="o")
                 for jj in range(size):
                     cols = slice(jj * A, (jj + 1) * A)
-                    nc.tensor.matmul(
-                        o[:, jj, :], lhsT=y[:, cols], rhs=ident[:], start=True, stop=False, is_transpose=True
-                    )
-                    nc.tensor.matmul(
-                        o[:, jj, :], lhsT=r[:, cols], rhs=ident[:], start=False, stop=True, is_transpose=True
-                    )
-                o_of[g] = o
+                    transpose_sum(turned[:, jj, :], y[:, cols], rest[:, cols])
+                out_of[g] = turned
 
-            last = len(GROUPS) - 1
-            for g in range(-2, len(GROUPS) + 3):
+            def store(g):
+                n, j0, size = groups[g][0:3]
+                result = work.tile([P, size, K1], F32, align_bytes=64, tag="result")
+                nc.scalar.copy(out=result[:], in_=out_of[g][:])
+                nc.sync.dma_start(out=out[n, :, j0 : j0 + size, :], in_=result[:])
+
+            for g in range(-2, last + 4):
                 if valid(g):
-                    h_of[g] = work.tile([P, GROUPS[g][2] * A, T], BF16, align_bytes=64, tag="h", name="h")
+                    h_of[g] = work.tile([P, groups[g][2] * A, T], BF16, align_bytes=64, tag="h", name="h")
                     z_back(g)
                 if valid(g + 2):
-                    z_planes(g + 2)
+                    nw, ns, nz = groups[g + 2][3:6]
+                    if nz:
+                        z_planes_of[g + 2] = w_planes(g + 2, nw + ns, nz, "z_planes")
                 if valid(g - 2):
-                    cols = GROUPS[g - 2][2] * A
-                    y = work.tile([P, cols], F32, align_bytes=64, tag="y")
-                    nc.scalar.activation(out=y[:], in_=x_of[g - 2][:], func=ACT.Identity, bias=b2c[:])
-                    r = work.tile([P, cols], F32, align_bytes=64, tag="r")
-                    if g - 2 >= last - 1:
-                        nc.vector.tensor_scalar(
-                            out=r[:], in0=y[:], scalar1=0.0, scalar2=-0.99, op0=ALU.min, op1=ALU.mult
-                        )
-                    else:
-                        nc.scalar.activation(out=r[:], in_=x_of[g - 2][:], func=ACT.Relu, bias=b2n[:], scale=-0.99)
-                    yr_of[g - 2] = (y, r)
+                    bias_and_rest(g - 2)
                 if valid(g - 3):
-                    n, j0, size = GROUPS[g - 3][0:3]
-                    o_sb = work.tile([P, size, K1], F32, align_bytes=64, tag="o_sb")
-                    nc.scalar.copy(out=o_sb[:], in_=o_of[g - 3][:])
-                    nc.sync.dma_start(out=out[n, :, j0 : j0 + size, :], in_=o_sb[:])
+                    store(g - 3)
                 if valid(g):
                     z_copy(g)
                 if valid(g + 1):
-                    z_add(g + 1)
+                    z_sums(g + 1)
+                    s_planes(g + 1)
                     z_round(g + 1)
-                    a_planes(g + 1)
                 if g == 1:
-                    nc.scalar.activation(out=t99[1][:], in_=a_ps[1][:], func=ACT.Copy, scale=0.99)
-                    nc.scalar.activation(out=t01[1][:], in_=a_ps[1][:], func=ACT.Copy, scale=0.01)
+                    nc.scalar.activation(out=a_high[1][:], in_=a_ps[1][:], func=ACT.Copy, scale=1.0 - SLOPE)
+                    nc.scalar.activation(out=a_low[1][:], in_=a_ps[1][:], func=ACT.Copy, scale=SLOPE)
+                    quantize(w2_codes, w2_scl, w2_grp)
                 if valid(g - 1):
-                    quantize_h(g - 1)
-                    x = psum.tile([P, GROUPS[g - 1][2] * A], F32, tag="x")
-                    for i in range(1):
-                        multiply_h(g - 1, x)
-                    x_of[g - 1] = x
+                    second_layer(g - 1)
                 if valid(g):
-                    nw = GROUPS[g][3]
+                    nw = groups[g][3]
                     if nw:
-                        ww = work.tile([P, T, nw * A], F32, align_bytes=64, tag="ww")
-                        max_add_planes(g, 0, nw, ww)
-                    if g == 0:
-                        nc.vector.quantize_mx(
-                            out=w2_codes[:].bitcast(FP8X4), scales=w2_scl[:], in_=w2_grp[:].rearrange("p e j -> p (e j)")
-                        )
-                    a_leaky(g)
-                    w_add(g, ww)
+                        planes = w_planes(g, 0, nw, "w_planes")
+                    s_leaky(g)
+                    if nw:
+                        w_sum(g, planes)
                 if valid(g - 2):
-                    out_transposes(g - 2)
-                    if False:
-                        junk = psum.tile([P, GROUPS[g - 2][2] * A], F32, tag="junk", bufs=1)
-                        for i in range(2):
-                            multiply_h(g - 2, junk)
+                    turn_output(g - 2)

from contextlib import ExitStack

import concourse.mybir as mybir
from concourse.masks import make_identity

B, A, C, D, K0, K1 = 2, 128, 64, 512, 512, 128
FLOPS = 2 * B * A * C * K0 * K1 + 2 * B * A * D * K0 + 2 * B * C * D * K0
SLOPE = 0.01

F32 = mybir.dt.float32
BF16 = mybir.dt.bfloat16
U32 = mybir.dt.uint32
U8 = mybir.dt.uint8
FP8 = mybir.dt.float8_e4m3fn
FP8X4 = mybir.dt.float8_e4m3fn_x4
ACT = mybir.ActivationFunctionType
ALU = mybir.AluOpType

P = 128
T = 4
RUN = 4
PLANE_GAP = 4

MIXTURES = {
    1: [(1, 0, 0), (0, 1, 0)],
    2: [(1, 1, 0)],
    4: [(2, 1, 1), (1, 2, 1)],
}
SIZES = {0: [1, 1, 2] + [4] * 15, 1: [4] * 15 + [2, 1, 1]}


def group_list():
    groups = []
    for n in range(B):
        j = 0
        for i, size in enumerate(SIZES[n]):
            mixtures = MIXTURES[size]
            groups.append((n, j, size) + mixtures[i % len(mixtures)])
            j += size
    return groups


def tile_matchmatrix_pa_t_kernel(tc, sent_a_bytes, sent_a_scale, sent_b, W1, b1, W2, b2, out):
    nc = tc.nc
    groups = group_list()
    last = len(groups) - 1

    with ExitStack() as ctx:
        keep = ctx.enter_context(tc.tile_pool(name="keep", bufs=1))
        head = ctx.enter_context(tc.tile_pool(name="head", bufs=T))
        work = ctx.enter_context(tc.tile_pool(name="work", bufs=3))
        psum = ctx.enter_context(tc.psum_pool(name="psum", bufs=2))

        a_bytes = keep.tile([P, B, D], U8, align_bytes=64)
        b_rows = keep.tile([P, D], BF16, align_bytes=64)
        a_scale = keep.tile([P, T], F32)
        wb_raw = keep.tile([P, T, K0], BF16, align_bytes=64)
        wa_raw = keep.tile([P, T, K0], BF16, align_bytes=64)
        w2_raw = keep.tile([P, T, K1], BF16, align_bytes=64)
        b1_cols = keep.tile([P, T], BF16)
        b2_col = keep.tile([P, 1], BF16)
        neg_b2 = keep.tile([P, 1], F32)
        ident = keep.tile([P, P], F32, align_bytes=64)
        dummy = keep.tile([P, 1], F32)

        a_wide = keep.tile([P, B, D], BF16, align_bytes=64)
        a_grp = keep.tile([P, B, A, T], BF16, align_bytes=64)
        b_grp = keep.tile([P, P, T], BF16, align_bytes=64)
        w2_grp = keep.tile([P, K1, T], BF16, align_bytes=64)
        a_codes = keep.tile([P, B * A], U32, align_bytes=64)
        a_scl = keep.tile([P, B * A], U8, align_bytes=64)
        b_codes = keep.tile([P, P], U32, align_bytes=64)
        b_scl = keep.tile([P, P], U8, align_bytes=64)
        w2_codes = keep.tile([P, K1], U32, align_bytes=64)
        w2_scl = keep.tile([P, K1], U8, align_bytes=64)

        b_plus = keep.tile([P, T, B * C], F32, align_bytes=64)
        b_neg = keep.tile([P, T, B * C], F32, align_bytes=64)
        a_low = []
        a_high = []
        for n in range(B):
            a_low.append(keep.tile([P, T, A], F32, align_bytes=64, name="a_low" + str(n)))
            a_high.append(keep.tile([P, T, A], F32, align_bytes=64, name="a_high" + str(n)))

        def quantize(codes, scl, grouped):
            nc.vector.quantize_mx(
                out=codes[:].bitcast(FP8X4), scales=scl[:], in_=grouped[:].rearrange("p c t -> p (c t)")
            )

        def multiply(out_ap, weights, rhs_codes, rhs_scl):
            nc.tensor.matmul_mx(
                out=out_ap,
                lhsT=weights[0][:].bitcast(FP8X4),
                lhsT_scale=weights[1][:],
                rhs=rhs_codes.bitcast(FP8X4),
                rhs_scale=rhs_scl,
                start=True,
                stop=True,
            )

        def transpose_sum(out_ap, first, second):
            nc.tensor.matmul(out_ap, lhsT=first, rhs=ident[:], start=True, stop=False, is_transpose=True)
            nc.tensor.matmul(out_ap, lhsT=second, rhs=ident[:], start=False, stop=True, is_transpose=True)

        with tc.manual_schedule():
            nc.scalar.dma_start(out=a_scale[:], in_=sent_a_scale.rearrange("x y (p t) -> p (x y t)", t=T))
            nc.sync.dma_start(out=a_bytes[:], in_=sent_a_bytes.rearrange("n i k -> i n k"))
            nc.sync.dma_start(out=b_rows[:], in_=sent_b.rearrange("n j k -> (n j) k"))
            nc.sync.dma_start(out=wb_raw[:], in_=W1[D : 2 * D, :].rearrange("(p t) c -> p t c", t=T))
            nc.sync.dma_start(out=wa_raw[:], in_=W1[0:D, :].rearrange("(p t) c -> p t c", t=T))
            nc.sync.dma_start(out=w2_raw[:], in_=W2.rearrange("(p t) e -> p t e", t=T))
            nc.scalar.dma_start(out=b1_cols[:], in_=b1.rearrange("(p t) -> p t", t=T))
            nc.scalar.dma_start(out=b2_col[:], in_=b2.rearrange("(e o) -> e o", o=1))
            nc.vector.memset(dummy[:], 0.0)
            nc.scalar.activation(out=dummy[:], in_=dummy[:], func=ACT.Identity)
            make_identity(nc, ident[:])

            at_ps = psum.tile([P, B, 2, A], F32, tag="hz")
            bt_ps = psum.tile([P, 2, P], F32, tag="hz")
            nc.vector.tensor_copy(out=a_wide[:, 0, :], in_=a_bytes[:, 0, :].bitcast(FP8))
            nc.scalar.activation(out=a_wide[:, 1, :], in_=a_bytes[:, 1, :].bitcast(FP8), func=ACT.Copy)
            a_words = a_wide[:].bitcast(F32)
            b_words = b_rows[:].bitcast(F32)
            for u in range(2):
                nc.tensor.transpose(bt_ps[:, u, :], b_words[:, u : D // 2 : 2], ident[:])
            for n in range(B):
                for u in range(2):
                    nc.tensor.transpose(at_ps[:, n, u, :], a_words[:, n, u : D // 2 : 2], ident[:])
            nc.scalar.copy(
                out=b_grp[:].rearrange("p r t -> p (r t)").bitcast(F32).rearrange("p (r u) -> p r u", u=2),
                in_=bt_ps[:].rearrange("p u r -> p r u"),
            )
            for n in range(B):
                nc.vector.tensor_tensor(
                    out=a_grp[:, n].rearrange("p i (u e) -> p i u e", u=2),
                    in0=at_ps[:, n].bitcast(BF16).rearrange("p u (i e) -> p i u e", e=2),
                    in1=a_scale[:].rearrange("p (u e) -> p u e", u=2).unsqueeze(1).to_broadcast([P, A, 2, 2]),
                    op=ALU.mult,
                )
            quantize(b_codes, b_scl, b_grp)
            nc.vector.quantize_mx(
                out=a_codes[:].bitcast(FP8X4), scales=a_scl[:], in_=a_grp[:].rearrange("p n i t -> p (n i t)")
            )
            nc.vector.tensor_scalar(out=neg_b2[:], in0=b2_col[:], scalar1=SLOPE - 1.0, scalar2=None, op0=ALU.mult)

            b_ps = psum.tile([P, T, B * C], F32, tag="x")
            a_ps = []
            for n in range(B):
                a_ps.append(psum.tile([P, T, A], F32, tag="o", name="a_ps" + str(n)))

            def weight_chunk(copy, raw, t, name):
                grouped = head.tile([P, P, T], BF16, align_bytes=64, name=name)
                copy(out=grouped[:], in_=raw[:].rearrange("p j (m t) -> p t m j", t=T)[:, t])
                return grouped

            def quantized_chunk(grouped, name):
                codes = head.tile([P, P], U32, align_bytes=64, name=name + "_codes")
                scl = head.tile([P, P], U8, align_bytes=64, name=name + "_scl")
                quantize(codes, scl, grouped)
                return codes, scl

            def a_multiply(n, t):
                cols = slice(n * A, (n + 1) * A)
                multiply(a_ps[n][:, t, :], wa_chunks[t], a_codes[:, cols], a_scl[:, cols])

            wb_grps = []
            for t in range(T):
                wb_grps.append(weight_chunk(nc.scalar.copy, wb_raw, t, "wb_grp"))
            wa_grps = []
            for t in range(T):
                copy = nc.scalar.copy if t == T - 1 else nc.vector.tensor_copy
                wa_grps.append(weight_chunk(copy, wa_raw, t, "wa_grp"))
                multiply(b_ps[:, t, :], quantized_chunk(wb_grps[t], "wb"), b_codes[:], b_scl[:])
            wa_chunks = []
            for t in range(T):
                wa_chunks.append(quantized_chunk(wa_grps[t], "wa"))
                a_multiply(0, t)
            for t in range(T):
                nc.vector.tensor_scalar(
                    out=b_plus[:, t, :], in0=b_ps[:, t, :], scalar1=b1_cols[:, t : t + 1], scalar2=None, op0=ALU.add
                )
                nc.scalar.activation(out=a_high[0][:, t, :], in_=a_ps[0][:, t, :], func=ACT.Copy, scale=1.0 - SLOPE)
            for t in range(T):
                a_multiply(1, t)
            nc.vector.tensor_scalar(out=b_neg[:], in0=b_plus[:], scalar1=SLOPE - 1.0, scalar2=None, op0=ALU.mult)
            nc.scalar.activation(out=a_low[0][:], in_=a_ps[0][:], func=ACT.Copy, scale=SLOPE)
            nc.scalar.copy(out=w2_grp[:], in_=w2_raw[:].rearrange("p t e -> p e t"))

            z_planes_of, z_sum_of, z_rows_of, z_words_of, s_planes_of = {}, {}, {}, {}, {}
            h_of, x_of, y_of, out_of = {}, {}, {}, {}

            def valid(g):
                return 0 <= g <= last

            def w_planes(g, first, count, tag):
                n, j0 = groups[g][0:2]
                planes = work.tile([P, T, count * A], F32, align_bytes=64, tag=tag, name=tag)
                for jj in range(count):
                    col = slice(n * C + j0 + first + jj, n * C + j0 + first + jj + 1)
                    for t in range(T):
                        nc.vector.tensor_scalar(
                            out=planes[:, t, jj * A : (jj + 1) * A],
                            in0=a_high[n][:, t, :],
                            scalar1=b_neg[:, t, col],
                            scalar2=b_plus[:, t, col],
                            op0=ALU.max,
                            op1=ALU.add,
                        )
                return planes

            def w_sum(g, planes):
                n, nw = groups[g][0], groups[g][3]
                for jj in range(nw):
                    cols = slice(jj * A, (jj + 1) * A)
                    nc.vector.tensor_tensor(
                        out=h_of[g][:, cols, :].rearrange("p (c i) t -> p c t i", i=RUN),
                        in0=a_low[n][:].rearrange("p t (c i) -> p c t i", i=RUN),
                        in1=planes[:, :, cols].rearrange("p t (c i) -> p c t i", i=RUN),
                        op=ALU.add,
                    )

            def s_planes(g):
                n, j0, size, nw, ns, nz = groups[g]
                if ns:
                    planes = work.tile([P, T, ns * A + PLANE_GAP], F32, align_bytes=64, tag="s_planes")
                    for jj in range(ns):
                        col = slice(n * C + j0 + nw + jj, n * C + j0 + nw + jj + 1)
                        for t in range(T):
                            nc.scalar.activation(
                                out=planes[:, t, jj * A : (jj + 1) * A],
                                in_=a_high[n][:, t, :],
                                func=ACT.Identity,
                                bias=b_plus[:, t, col],
                                scale=1.0 / (1.0 - SLOPE),
                            )
                    s_planes_of[g] = planes

            def s_leaky(g):
                n, j0, size, nw, ns, nz = groups[g]
                if ns:
                    v = s_planes_of[g][:, :, 0 : ns * A].rearrange("p t c -> p c t")
                    nc.vector.scalar_tensor_tensor(
                        out=h_of[g][:, nw * A : (nw + ns) * A, :], in0=v, scalar=SLOPE, in1=v, op0=ALU.mult, op1=ALU.max
                    )

            def z_sums(g):
                n, nz = groups[g][0], groups[g][5]
                for jz in range(nz):
                    z_sum = psum.tile([P, T, P], F32, tag="hz")
                    for t in range(T):
                        w = z_planes_of[g][:, t, jz * A : (jz + 1) * A]
                        transpose_sum(z_sum[:, t, :], w, a_low[n][:, t, :])
                    z_sum_of[g, jz] = z_sum

            def z_round(g):
                for jz in range(groups[g][5]):
                    rows = work.tile([P, 2, P, 2], BF16, align_bytes=64, tag="z_rows")
                    nc.scalar.copy(out=rows[:], in_=z_sum_of[g, jz][:].rearrange("i (u e) m -> i u m e", e=2))
                    z_rows_of[g, jz] = rows

            def z_back(g):
                nz = groups[g][5]
                if nz:
                    words = psum.tile([P, nz, 2, A], F32, tag="words", bufs=1)
                    for jz in range(nz):
                        rows = z_rows_of[g, jz][:].rearrange("i u m e -> i (u m e)").bitcast(F32)
                        for u in range(2):
                            nc.tensor.transpose(words[:, jz, u, :], rows[:, u * P : (u + 1) * P], ident[:])
                    z_words_of[g] = words

            def z_copy(g):
                n, j0, size, nw, ns, nz = groups[g]
                if nz:
                    h_words = h_of[g][:, (nw + ns) * A :, :].rearrange("p c t -> p (c t)").bitcast(F32)
                    nc.scalar.copy(
                        out=h_words.rearrange("p (j i u) -> p j i u", j=nz, u=2),
                        in_=z_words_of[g][:].rearrange("p j u i -> p j i u"),
                    )

            def second_layer(g):
                cols = groups[g][2] * A
                h_codes = work.tile([P, cols], U32, align_bytes=64, tag="h_codes")
                h_scl = work.tile([P, cols], U8, align_bytes=64, tag="h_scl")
                quantize(h_codes, h_scl, h_of[g])
                x = psum.tile([P, cols], F32, tag="x")
                multiply(x[:], (w2_codes, w2_scl), h_codes[:], h_scl[:])
                x_of[g] = x

            def bias_and_rest(g):
                cols = groups[g][2] * A
                y = work.tile([P, cols], F32, align_bytes=64, tag="y")
                nc.scalar.activation(out=y[:], in_=x_of[g][:], func=ACT.Identity, bias=b2_col[:])
                rest = work.tile([P, cols], F32, align_bytes=64, tag="rest")
                if g >= last - 1:
                    nc.vector.tensor_scalar(
                        out=rest[:], in0=y[:], scalar1=0.0, scalar2=SLOPE - 1.0, op0=ALU.min, op1=ALU.mult
                    )
                else:
                    nc.scalar.activation(
                        out=rest[:], in_=x_of[g][:], func=ACT.Relu, bias=neg_b2[:], scale=SLOPE - 1.0
                    )
                y_of[g] = (y, rest)

            def turn_output(g):
                y, rest = y_of[g]
                size = groups[g][2]
                turned = psum.tile([P, size, K1], F32, tag="o")
                for jj in range(size):
                    cols = slice(jj * A, (jj + 1) * A)
                    transpose_sum(turned[:, jj, :], y[:, cols], rest[:, cols])
                out_of[g] = turned

            def store(g):
                n, j0, size = groups[g][0:3]
                result = work.tile([P, size, K1], F32, align_bytes=64, tag="result")
                nc.scalar.copy(out=result[:], in_=out_of[g][:])
                nc.sync.dma_start(out=out[n, :, j0 : j0 + size, :], in_=result[:])

            for g in range(-2, last + 4):
                if valid(g):
                    h_of[g] = work.tile([P, groups[g][2] * A, T], BF16, align_bytes=64, tag="h", name="h")
                    z_back(g)
                if valid(g + 2):
                    nw, ns, nz = groups[g + 2][3:6]
                    if nz:
                        z_planes_of[g + 2] = w_planes(g + 2, nw + ns, nz, "z_planes")
                if valid(g - 2):
                    bias_and_rest(g - 2)
                if valid(g - 3):
                    store(g - 3)
                if valid(g):
                    z_copy(g)
                if valid(g + 1):
                    z_sums(g + 1)
                    s_planes(g + 1)
                    z_round(g + 1)
                if g == 1:
                    nc.scalar.activation(out=a_high[1][:], in_=a_ps[1][:], func=ACT.Copy, scale=1.0 - SLOPE)
                    nc.scalar.activation(out=a_low[1][:], in_=a_ps[1][:], func=ACT.Copy, scale=SLOPE)
                    quantize(w2_codes, w2_scl, w2_grp)
                if valid(g - 1):
                    second_layer(g - 1)
                if valid(g):
                    nw = groups[g][3]
                    if nw:
                        planes = w_planes(g, 0, nw, "w_planes")
                    s_leaky(g)
                    if nw:
                        w_sum(g, planes)
                if valid(g - 2):
                    turn_output(g - 2)
